import numpy as np
import ml_dtypes


def mxq(x, axis, fmt="e4m3"):
    dtype, down = {"e4m3": (ml_dtypes.float8_e4m3fn, 7), "e5m2": (ml_dtypes.float8_e5m2, 14)}[fmt]
    v = np.moveaxis(np.asarray(x, np.float32).astype(ml_dtypes.bfloat16).astype(np.float64), axis, -1)
    blocks = v.reshape(v.shape[:-1] + (-1, 32))
    amax = np.abs(blocks).max(-1, keepdims=True)
    byte = np.maximum(np.where(amax > 0, np.frexp(amax)[1] - 1 + 127, 0) - down, 1)
    scale = np.exp2(byte - 127.0)
    codes = (blocks / scale).astype(np.float32).astype(dtype).astype(np.float64)
    return np.moveaxis((codes * scale).reshape(v.shape), -1, axis)


WIDE = False


def mx_kscale(k):
    if not WIDE:
        return np.ones(k)
    levels = np.array([10, -10, 5, -5, 0])
    a = np.random.permutation(np.resize(levels, k // 512 * 4)).reshape(k // 512, 4)
    idx = np.arange(k)
    return np.exp2(a[idx // 512, idx % 128 // 32])


BF16 = ml_dtypes.bfloat16


def bf(x):
    return np.asarray(x, np.float32).astype(BF16)


def f64(x):
    return np.asarray(x).astype(np.float64)


E2M1 = np.array([0.0, 0.5, 1.0, 1.5, 2.0, 3.0, 4.0, 6.0, -0.0, -0.5, -1.0, -1.5, -2.0, -3.0, -4.0, -6.0])


def pack_weight(w, fmt):
    k, n = w.shape
    w = f64(bf(w)).reshape(k // 32, 32, n)
    amax = np.abs(w).max(1)
    if fmt == "e4m3":
        byte = np.frexp(amax)[1] - 1 + 127 - 7
    else:
        mant, ex = np.frexp(amax / 6.0)
        byte = np.where(mant > 0.5, ex, ex - 1) + 127
    byte = np.clip(np.where(amax > 0, byte, 1), 1, 254)
    scaled = (w * np.exp2(127.0 - byte)[:, None, :]).reshape(k, n).astype(np.float32)
    by_word = np.ascontiguousarray(scaled.reshape(k // 512, 128, 4, n).transpose(0, 1, 3, 2))
    if fmt == "e4m3":
        words = by_word.astype(ml_dtypes.float8_e4m3fn).view(np.uint8)
    else:
        c = by_word.astype(ml_dtypes.float4_e2m1fn).view(np.uint8) & 0xF
        words = c[..., 0::2] | (c[..., 1::2] << 4)
    return np.ascontiguousarray(words), np.ascontiguousarray(byte.astype(np.uint8).reshape(k // 512, 16, n))


def unpack_weight(words, scales, fmt):
    g, p, n, _ = words.shape
    if fmt == "e4m3":
        vals = np.ascontiguousarray(words).view(ml_dtypes.float8_e4m3fn).astype(np.float64)
    else:
        nib = np.empty((g, p, n, 4), np.uint8)
        nib[..., 0::2] = words & 0xF
        nib[..., 1::2] = words >> 4
        vals = E2M1[nib]
    vals = vals * np.repeat(np.exp2(scales.astype(np.float64) - 127.0), 8, axis=1)[..., None]
    return vals.transpose(0, 1, 3, 2).reshape(g * 512, n)


B, N, D0, D1, D2, D3 = 64, 128, 512, 512, 512, 1024
EPS = 1e-5


def batch_norm(x, g, b):
    mean = x.mean(axis=(0, 1))
    var = np.square(x - mean).mean(axis=(0, 1))
    return (x - mean) * (1.0 / np.sqrt(var + EPS)) * g + b


def setup_inputs():
    s = mx_kscale(D0)
    feats = np.random.standard_normal((B, N, D0)) * np.exp(0.4 * np.random.standard_normal(D0)) + 0.5 * np.random.standard_normal(D0)
    g0 = bf((1.0 + 0.2 * np.random.standard_normal(D0)) * s)
    b0 = bf(0.2 * np.random.standard_normal(D0) * s)
    W0 = np.random.standard_normal((D1, D0)) / np.sqrt(D0) / s
    W0_words, W0_scales = pack_weight(W0.T, "e4m3")
    return {"set_feats": bf(feats),
            "g0": g0,
            "b0": b0,
            "W0_words": W0_words,
            "W0_scales": W0_scales,
            "c0": bf(0.3 * np.random.standard_normal(D1)),
            "g1": bf(1.0 + 0.2 * np.random.standard_normal(D1)),
            "b1": bf(0.2 * np.random.standard_normal(D1))}


def reference(set_feats, g0, b0, W0_words, W0_scales, c0, g1, b1):
    x0 = batch_norm(f64(set_feats), f64(g0), f64(b0))
    h0 = np.maximum((mxq(x0, 2, "e4m3") @ unpack_weight(W0_words, W0_scales, "e4m3")) + f64(c0), 0.0)
    return batch_norm(h0, f64(g1), f64(b1))

@@ -1,0 +1,232 @@
+import concourse.mybir as mybir
+from concourse.masks import make_identity
+
+FLOPS = 2 * 8192 * 512 * 512
+
+F32 = mybir.dt.float32
+BF16 = mybir.dt.bfloat16
+I32 = mybir.dt.int32
+U32 = mybir.dt.uint32
+U8 = mybir.dt.uint8
+FP8X4 = mybir.dt.float8_e4m3fn_x4
+ALU = mybir.AluOpType
+ACT = mybir.ActivationFunctionType
+
+P = 128
+PACK = 4
+HALVES = 2
+WORDS = PACK // HALVES
+ROWS = 8192
+K = 512
+N_OUT = 512
+N_CHUNKS = N_OUT // P
+ROW_TILES = ROWS // P
+EPS = 1e-5
+
+LOAD_TILES = 8
+BANK_TILES = 2
+BANK_ROWS = BANK_TILES * P
+STAT_WIDTH = 6
+ENTRY = 3
+
+GROUP = 512
+GROUP_TILES = GROUP // P
+GROUPS = ROWS // GROUP
+RUN = 4
+
+SQUARE_GROUPS = 10
+SQUARE_SPAN = 2
+SQUARES = SQUARE_GROUPS // SQUARE_SPAN
+BN_GROUPS = GROUPS - SQUARE_GROUPS
+
+VECTOR_EVERY = 4
+
+
+def norm_coefficients(nc, pool, mean_var, gain, shift_in, label):
+    width = gain.shape[1]
+    rstd = pool.tile([P, width], F32, name="rstd" + label)
+    scale = pool.tile([P, width], F32, name="scale" + label)
+    shift = pool.tile([P, width], F32, name="shift" + label)
+    nc.vector.tensor_scalar(out=rstd[:], in0=mean_var[:, :, 1], scalar1=EPS, scalar2=None, op0=ALU.add)
+    nc.scalar.sqrt(out=rstd[:], in_=rstd[:])
+    nc.vector.reciprocal(out=rstd[:], in_=rstd[:])
+    nc.vector.tensor_tensor(out=scale[:], in0=rstd[:], in1=gain, op=ALU.mult)
+    nc.vector.tensor_tensor(out=shift[:], in0=mean_var[:, :, 0], in1=scale[:], op=ALU.mult)
+    nc.vector.tensor_tensor(out=shift[:], in0=shift_in, in1=shift[:], op=ALU.subtract)
+    return scale, shift
+
+
+def tile_settransform_pa_kernel(tc, set_feats, g0, b0, W0_words, W0_scales, c0, g1, b1, out):
+    nc = tc.nc
+    x_rows = set_feats.rearrange("b s k -> (b s) k").rearrange("(p j) k -> p j k", j=ROW_TILES)
+    out_rows = out.rearrange("b s n -> (b s) n").rearrange("(p j) n -> p j n", j=ROW_TILES)
+
+    with tc.tile_pool(name="const", bufs=1) as const, tc.tile_pool(name="hidden", bufs=1) as hidden:
+        identity = const.tile([P, P], F32)
+        make_identity(nc, identity[:])
+
+        warm = const.tile([P, 1], F32)
+        nc.vector.memset(warm[:], 1.0)
+        nc.scalar.sqrt(out=warm[:], in_=warm[:])
+
+        w_words = const.tile([P, N_OUT], U32, align_bytes=64)
+        w_plane = const.tile([P, N_OUT], U8, align_bytes=64)
+        nc.vector.memset(w_plane[:].bitcast(I32), 0)
+
+        h0T = hidden.tile([P, N_CHUNKS, ROWS], F32)
+
+        with tc.tile_pool(name="xT", bufs=1) as xT_pool:
+            xT = xT_pool.tile([P, WORDS, ROWS], F32)
+
+            stats0 = const.tile([P, WORDS, ROWS // BANK_ROWS, STAT_WIDTH], F32)
+            with tc.tile_pool(name="load", bufs=3) as load, tc.psum_pool(name="psumA", bufs=4) as psum_a:
+                for first in range(0, ROW_TILES, LOAD_TILES):
+                    x_sb = load.tile([P, LOAD_TILES, K], BF16, name="x_sb")
+                    nc.sync.dma_start(out=x_sb[:], in_=x_rows[:, first : first + LOAD_TILES, :])
+                    for pair in range(0, LOAD_TILES, BANK_TILES):
+                        bank = (first + pair) // BANK_TILES
+                        cols = slice(bank * BANK_ROWS, (bank + 1) * BANK_ROWS)
+                        flipped = psum_a.tile([P, WORDS, BANK_ROWS], F32, name="flipped")
+                        for u in range(WORDS):
+                            for i in range(BANK_TILES):
+                                words = x_sb[:, pair + i, :].bitcast(F32)
+                                nc.tensor.transpose(
+                                    flipped[:, u, i * P : (i + 1) * P], words[:, u : K // HALVES : WORDS], identity[:]
+                                )
+                        nc.scalar.copy(out=xT[:, :, cols], in_=flipped[:])
+                        for u in range(WORDS):
+                            nc.vector.bn_stats(out=stats0[:, u, bank, :], in_=xT[:, u, cols].bitcast(BF16))
+
+                nc.sync.dma_start(
+                    out=w_words[:].bitcast(I32), in_=W0_words[0].rearrange("p n t -> p (n t)").bitcast(I32)
+                )
+                for quadrant in range(4):
+                    nc.sync.dma_start(
+                        out=w_plane[32 * quadrant : 32 * quadrant + 4, :].bitcast(I32),
+                        in_=W0_scales[0, 4 * quadrant : 4 * quadrant + 4, :].bitcast(I32),
+                    )
+                vectors_bf = const.tile([P, 5, 16], BF16)
+                vectors = const.tile([P, 5, PACK], F32)
+                with nc.allow_non_contiguous_dma(reason="five vectors of 512 values, four to a partition"):
+                    nc.sync.dma_start(out=vectors_bf[:, 0, 0:PACK], in_=g0.rearrange("(p t) -> p t", t=PACK))
+                    nc.sync.dma_start(out=vectors_bf[:, 1, 0:PACK], in_=b0.rearrange("(p t) -> p t", t=PACK))
+                    nc.sync.dma_start(out=vectors_bf[:, 2, 0:N_CHUNKS], in_=c0.rearrange("(c p) -> p c", p=P))
+                    nc.sync.dma_start(out=vectors_bf[:, 3, 0:N_CHUNKS], in_=g1.rearrange("(c p) -> p c", p=P))
+                    nc.sync.dma_start(out=vectors_bf[:, 4, 0:N_CHUNKS], in_=b1.rearrange("(c p) -> p c", p=P))
+                nc.vector.tensor_copy(out=vectors[:], in_=vectors_bf[:, :, 0:PACK])
+
+                mean_var0 = const.tile([P, PACK, 2], F32)
+                for u in range(WORDS):
+                    for e in range(HALVES):
+                        nc.vector.bn_aggr(
+                            out=mean_var0[:, HALVES * u + e, :], in_=stats0[:, u, :, ENTRY * e : ENTRY * (e + 1)]
+                        )
+                scale0, shift0 = norm_coefficients(nc, const, mean_var0, vectors[:, 0, :], vectors[:, 1, :], "0")
+
+            relu_sums = const.tile([P, N_CHUNKS, SQUARE_GROUPS], F32)
+            square_sums = const.tile([P, N_CHUNKS, SQUARES], F32)
+            stats1 = const.tile([P, N_CHUNKS, BN_GROUPS * STAT_WIDTH + ENTRY], F32)
+            with tc.tile_pool(name="work", bufs=2) as work, tc.psum_pool(name="psumB", bufs=8) as psum_b:
+                for g in range(GROUPS):
+                    cols = slice(g * GROUP, (g + 1) * GROUP)
+                    planes = work.tile([P, PACK, GROUP], BF16, name="planes")
+                    for u in range(WORDS):
+                        halves = xT[:, u, cols].bitcast(BF16).rearrange("p (r e) -> p r e", e=HALVES)
+                        for e in range(HALVES):
+                            t = HALVES * u + e
+                            nc.vector.tensor_scalar(
+                                out=planes[:, t, :],
+                                in0=halves[:, :, e],
+                                scalar1=scale0[:, t : t + 1],
+                                scalar2=shift0[:, t : t + 1],
+                                op0=ALU.mult,
+                                op1=ALU.add,
+                            )
+                    grouped = work.tile([P, GROUP, PACK], BF16, name="grouped", align_bytes=64)
+                    nc.vector.tensor_copy(
+                        out=grouped[:].rearrange("p (c i) t -> p c t i", i=RUN),
+                        in_=planes[:].rearrange("p t (c i) -> p c t i", i=RUN),
+                    )
+                    codes = work.tile([P, GROUP], U32, name="codes", align_bytes=64)
+                    x_plane = work.tile([P, GROUP], U8, name="x_plane", align_bytes=64)
+                    nc.vector.quantize_mx(
+                        out=codes[:].bitcast(FP8X4), scales=x_plane[:], in_=grouped[:].rearrange("p r t -> p (r t)")
+                    )
+                    for c in range(N_CHUNKS):
+                        n_cols = slice(c * P, (c + 1) * P)
+                        acc = psum_b.tile([P, GROUP], F32, name="acc")
+                        nc.tensor.matmul_mx(
+                            out=acc[:],
+                            lhsT=w_words[:, n_cols].bitcast(FP8X4),
+                            lhsT_scale=w_plane[:, n_cols],
+                            rhs=codes[:].bitcast(FP8X4),
+                            rhs_scale=x_plane[:],
+                            start=True,
+                            stop=True,
+                        )
+                        if g < SQUARE_GROUPS:
+                            nc.scalar.activation(
+                                out=h0T[:, c, cols],
+                                in_=acc[:],
+                                func=ACT.Relu,
+                                bias=vectors[:, 2, c : c + 1],
+                                scale=1.0,
+                                accum_out=relu_sums[:, c, g : g + 1],
+                            )
+                        else:
+                            nc.scalar.activation(
+                                out=h0T[:, c, cols], in_=acc[:], func=ACT.Relu, bias=vectors[:, 2, c : c + 1], scale=1.0
+                            )
+                            entry = (g - SQUARE_GROUPS) * STAT_WIDTH
+                            nc.vector.bn_stats(out=stats1[:, c, entry : entry + STAT_WIDTH], in_=h0T[:, c, cols])
+                    if g < SQUARE_GROUPS and g % SQUARE_SPAN == SQUARE_SPAN - 1:
+                        span = slice((g + 1 - SQUARE_SPAN) * GROUP, (g + 1) * GROUP)
+                        for c in range(N_CHUNKS):
+                            unread = work.tile([P, SQUARE_SPAN * GROUP], BF16, name="unread")
+                            nc.scalar.activation(
+                                out=unread[:],
+                                in_=h0T[:, c, span],
+                                func=ACT.Square,
+                                accum_out=square_sums[:, c, g // SQUARE_SPAN : g // SQUARE_SPAN + 1],
+                            )
+
+                count = float(SQUARE_GROUPS * GROUP)
+                last = BN_GROUPS * STAT_WIDTH
+                total = const.tile([P, N_CHUNKS], F32)
+                total_sq = const.tile([P, N_CHUNKS], F32)
+                nc.vector.tensor_reduce(out=total[:], in_=relu_sums[:], axis=mybir.AxisListType.X, op=ALU.add)
+                nc.vector.tensor_reduce(out=total_sq[:], in_=square_sums[:], axis=mybir.AxisListType.X, op=ALU.add)
+                nc.vector.memset(stats1[:, :, last], count)
+                nc.vector.tensor_scalar(
+                    out=stats1[:, :, last + 1], in0=total[:], scalar1=1.0 / count, scalar2=None, op0=ALU.mult
+                )
+                nc.vector.tensor_tensor(out=total[:], in0=total[:], in1=stats1[:, :, last + 1], op=ALU.mult)
+                nc.vector.tensor_tensor(out=stats1[:, :, last + 2], in0=total_sq[:], in1=total[:], op=ALU.subtract)
+                mean_var1 = const.tile([P, N_CHUNKS, 2], F32)
+                for c in range(N_CHUNKS):
+                    nc.vector.bn_aggr(out=mean_var1[:, c, :], in_=stats1[:, c, :])
+                scale1, shift1 = norm_coefficients(nc, const, mean_var1, vectors[:, 3, :], vectors[:, 4, :], "1")
+
+        with tc.tile_pool(name="stage", bufs=4) as stage, tc.psum_pool(name="psumC", bufs=6) as psum_c:
+            for g in range(GROUPS):
+                cols = slice(g * GROUP, (g + 1) * GROUP)
+                for c in range(N_CHUNKS):
+                    nc.vector.tensor_scalar(
+                        out=h0T[:, c, cols],
+                        in0=h0T[:, c, cols],
+                        scalar1=scale1[:, c : c + 1],
+                        scalar2=shift1[:, c : c + 1],
+                        op0=ALU.mult,
+                        op1=ALU.add,
+                    )
+                result = stage.tile([P, GROUP_TILES, N_OUT], F32, name="result")
+                for i in range(GROUP_TILES):
+                    j = g * GROUP_TILES + i
+                    back = psum_c.tile([P, N_OUT], F32, name="back")
+                    for c in range(N_CHUNKS):
+                        nc.tensor.transpose(back[:, c * P : (c + 1) * P], h0T[:, c, j * P : (j + 1) * P], identity[:])
+                    if j % VECTOR_EVERY == 0:
+                        nc.vector.tensor_copy(out=result[:, i, :], in_=back[:])
+                    else:
+                        nc.scalar.copy(out=result[:, i, :], in_=back[:])
+                nc.sync.dma_start(out=out_rows[:, g * GROUP_TILES : (g + 1) * GROUP_TILES, :], in_=result[:])

@@ -26,18 +26,17 @@ EPS = 1e-5
 LOAD_TILES = 8
 BANK_TILES = 2
 BANK_ROWS = BANK_TILES * P
+STAT_ROWS = 512
 STAT_WIDTH = 6
-ENTRY = 3
 
 GROUP = 512
 GROUP_TILES = GROUP // P
 GROUPS = ROWS // GROUP
+NORM_GROUPS = 4
 RUN = 4
 
-SQUARE_GROUPS = 10
+SUM_CHUNKS = 2
 SQUARE_SPAN = 2
-SQUARES = SQUARE_GROUPS // SQUARE_SPAN
-BN_GROUPS = GROUPS - SQUARE_GROUPS
 
 VECTOR_EVERY = 4
 
@@ -61,7 +60,7 @@ def tile_settransform_pa_kernel(tc, set_feats, g0, b0, W0_words, W0_scales, c0, 
     x_rows = set_feats.rearrange("b s k -> (b s) k").rearrange("(p j) k -> p j k", j=ROW_TILES)
     out_rows = out.rearrange("b s n -> (b s) n").rearrange("(p j) n -> p j n", j=ROW_TILES)
 
-    with tc.tile_pool(name="const", bufs=1) as const, tc.tile_pool(name="hidden", bufs=1) as hidden:
+    with tc.manual_schedule(), tc.tile_pool(name="const", bufs=1) as const, tc.tile_pool(name="hidden", bufs=1) as hidden:
         identity = const.tile([P, P], F32)
         make_identity(nc, identity[:])
 
@@ -76,16 +75,15 @@ def tile_settransform_pa_kernel(tc, set_feats, g0, b0, W0_words, W0_scales, c0, 
         h0T = hidden.tile([P, N_CHUNKS, ROWS], F32)
 
         with tc.tile_pool(name="xT", bufs=1) as xT_pool:
-            xT = xT_pool.tile([P, WORDS, ROWS], F32)
+            xT = xT_pool.tile([P, PACK, ROWS], BF16)
 
-            stats0 = const.tile([P, WORDS, ROWS // BANK_ROWS, STAT_WIDTH], F32)
-            with tc.tile_pool(name="load", bufs=3) as load, tc.psum_pool(name="psumA", bufs=4) as psum_a:
+            stats0 = const.tile([P, PACK, ROWS // STAT_ROWS, STAT_WIDTH], F32)
+            with tc.tile_pool(name="load", bufs=4) as load, tc.psum_pool(name="psumA", bufs=4) as psum_a:
                 for first in range(0, ROW_TILES, LOAD_TILES):
                     x_sb = load.tile([P, LOAD_TILES, K], BF16, name="x_sb")
                     nc.sync.dma_start(out=x_sb[:], in_=x_rows[:, first : first + LOAD_TILES, :])
                     for pair in range(0, LOAD_TILES, BANK_TILES):
-                        bank = (first + pair) // BANK_TILES
-                        cols = slice(bank * BANK_ROWS, (bank + 1) * BANK_ROWS)
+                        start_row = (first + pair) * P
                         flipped = psum_a.tile([P, WORDS, BANK_ROWS], F32, name="flipped")
                         for u in range(WORDS):
                             for i in range(BANK_TILES):
@@ -93,9 +91,16 @@ def tile_settransform_pa_kernel(tc, set_feats, g0, b0, W0_words, W0_scales, c0, 
                                 nc.tensor.transpose(
                                     flipped[:, u, i * P : (i + 1) * P], words[:, u : K // HALVES : WORDS], identity[:]
                                 )
-                        nc.scalar.copy(out=xT[:, :, cols], in_=flipped[:])
-                        for u in range(WORDS):
-                            nc.vector.bn_stats(out=stats0[:, u, bank, :], in_=xT[:, u, cols].bitcast(BF16))
+                        nc.scalar.copy(
+                            out=xT[:, :, start_row : start_row + BANK_ROWS].rearrange("p (u e) r -> p u e r", e=HALVES),
+                            in_=flipped[:].bitcast(BF16).rearrange("p u (r e) -> p u e r", e=HALVES),
+                        )
+                        if (start_row + BANK_ROWS) % STAT_ROWS == 0:
+                            piece = start_row // STAT_ROWS
+                            for t in range(PACK):
+                                nc.vector.bn_stats(
+                                    out=stats0[:, t, piece, :], in_=xT[:, t, piece * STAT_ROWS : (piece + 1) * STAT_ROWS]
+                                )
 
                 nc.sync.dma_start(
                     out=w_words[:].bitcast(I32), in_=W0_words[0].rearrange("p n t -> p (n t)").bitcast(I32)
@@ -116,42 +121,49 @@ def tile_settransform_pa_kernel(tc, set_feats, g0, b0, W0_words, W0_scales, c0, 
                 nc.vector.tensor_copy(out=vectors[:], in_=vectors_bf[:, :, 0:PACK])
 
                 mean_var0 = const.tile([P, PACK, 2], F32)
-                for u in range(WORDS):
-                    for e in range(HALVES):
-                        nc.vector.bn_aggr(
-                            out=mean_var0[:, HALVES * u + e, :], in_=stats0[:, u, :, ENTRY * e : ENTRY * (e + 1)]
-                        )
+                for t in range(PACK):
+                    nc.vector.bn_aggr(out=mean_var0[:, t, :], in_=stats0[:, t, :, :].rearrange("p a b -> p (a b)"))
                 scale0, shift0 = norm_coefficients(nc, const, mean_var0, vectors[:, 0, :], vectors[:, 1, :], "0")
 
-            relu_sums = const.tile([P, N_CHUNKS, SQUARE_GROUPS], F32)
-            square_sums = const.tile([P, N_CHUNKS, SQUARES], F32)
-            stats1 = const.tile([P, N_CHUNKS, BN_GROUPS * STAT_WIDTH + ENTRY], F32)
+            relu_sums = const.tile([P, SUM_CHUNKS, GROUPS], F32)
+            square_sums = const.tile([P, SUM_CHUNKS, GROUPS // SQUARE_SPAN], F32)
+            stats1 = const.tile([P, N_CHUNKS - SUM_CHUNKS, GROUPS, STAT_WIDTH], F32)
             with tc.tile_pool(name="work", bufs=2) as work, tc.psum_pool(name="psumB", bufs=8) as psum_b:
-                for g in range(GROUPS):
-                    cols = slice(g * GROUP, (g + 1) * GROUP)
-                    planes = work.tile([P, PACK, GROUP], BF16, name="planes")
-                    for u in range(WORDS):
-                        halves = xT[:, u, cols].bitcast(BF16).rearrange("p (r e) -> p r e", e=HALVES)
-                        for e in range(HALVES):
-                            t = HALVES * u + e
-                            nc.vector.tensor_scalar(
-                                out=planes[:, t, :],
-                                in0=halves[:, :, e],
-                                scalar1=scale0[:, t : t + 1],
-                                scalar2=shift0[:, t : t + 1],
-                                op0=ALU.mult,
-                                op1=ALU.add,
-                            )
+                grouped_of = {}
+                codes_of = {}
+
+                def first_norm(g):
+                    cols = slice(g * GROUP, (g + NORM_GROUPS) * GROUP)
+                    for t in range(PACK):
+                        nc.vector.tensor_scalar(
+                            out=xT[:, t, cols],
+                            in0=xT[:, t, cols],
+                            scalar1=scale0[:, t : t + 1],
+                            scalar2=shift0[:, t : t + 1],
+                            op0=ALU.mult,
+                            op1=ALU.add,
+                        )
+
+                def regroup(g):
                     grouped = work.tile([P, GROUP, PACK], BF16, name="grouped", align_bytes=64)
                     nc.vector.tensor_copy(
                         out=grouped[:].rearrange("p (c i) t -> p c t i", i=RUN),
-                        in_=planes[:].rearrange("p t (c i) -> p c t i", i=RUN),
+                        in_=xT[:, :, g * GROUP : (g + 1) * GROUP].rearrange("p t (c i) -> p c t i", i=RUN),
                     )
+                    grouped_of[g] = grouped
+
+                def quantise(g):
                     codes = work.tile([P, GROUP], U32, name="codes", align_bytes=64)
                     x_plane = work.tile([P, GROUP], U8, name="x_plane", align_bytes=64)
                     nc.vector.quantize_mx(
-                        out=codes[:].bitcast(FP8X4), scales=x_plane[:], in_=grouped[:].rearrange("p r t -> p (r t)")
+                        out=codes[:].bitcast(FP8X4),
+                        scales=x_plane[:],
+                        in_=grouped_of[g][:].rearrange("p r t -> p (r t)"),
                     )
+                    codes_of[g] = (codes, x_plane)
+
+                def multiply(g):
+                    codes, x_plane = codes_of[g]
                     for c in range(N_CHUNKS):
                         n_cols = slice(c * P, (c + 1) * P)
                         acc = psum_b.tile([P, GROUP], F32, name="acc")
@@ -164,51 +176,68 @@ def tile_settransform_pa_kernel(tc, set_feats, g0, b0, W0_words, W0_scales, c0, 
                             start=True,
                             stop=True,
                         )
-                        if g < SQUARE_GROUPS:
-                            nc.scalar.activation(
-                                out=h0T[:, c, cols],
-                                in_=acc[:],
-                                func=ACT.Relu,
-                                bias=vectors[:, 2, c : c + 1],
-                                scale=1.0,
-                                accum_out=relu_sums[:, c, g : g + 1],
-                            )
-                        else:
-                            nc.scalar.activation(
-                                out=h0T[:, c, cols], in_=acc[:], func=ACT.Relu, bias=vectors[:, 2, c : c + 1], scale=1.0
-                            )
-                            entry = (g - SQUARE_GROUPS) * STAT_WIDTH
-                            nc.vector.bn_stats(out=stats1[:, c, entry : entry + STAT_WIDTH], in_=h0T[:, c, cols])
-                    if g < SQUARE_GROUPS and g % SQUARE_SPAN == SQUARE_SPAN - 1:
-                        span = slice((g + 1 - SQUARE_SPAN) * GROUP, (g + 1) * GROUP)
-                        for c in range(N_CHUNKS):
+                        nc.scalar.activation(
+                            out=h0T[:, c, g * GROUP : (g + 1) * GROUP],
+                            in_=acc[:],
+                            func=ACT.Relu,
+                            bias=vectors[:, 2, c : c + 1],
+                            scale=1.0,
+                            accum_out=relu_sums[:, c, g : g + 1] if c < SUM_CHUNKS else None,
+                        )
+
+                def hidden_statistics(g):
+                    for c in range(SUM_CHUNKS, N_CHUNKS):
+                        nc.vector.bn_stats(
+                            out=stats1[:, c - SUM_CHUNKS, g, :], in_=h0T[:, c, g * GROUP : (g + 1) * GROUP]
+                        )
+                    if g % SQUARE_SPAN == SQUARE_SPAN - 1:
+                        for c in range(SUM_CHUNKS):
                             unread = work.tile([P, SQUARE_SPAN * GROUP], BF16, name="unread")
                             nc.scalar.activation(
                                 out=unread[:],
-                                in_=h0T[:, c, span],
+                                in_=h0T[:, c, (g + 1 - SQUARE_SPAN) * GROUP : (g + 1) * GROUP],
                                 func=ACT.Square,
                                 accum_out=square_sums[:, c, g // SQUARE_SPAN : g // SQUARE_SPAN + 1],
                             )
 
-                count = float(SQUARE_GROUPS * GROUP)
-                last = BN_GROUPS * STAT_WIDTH
-                total = const.tile([P, N_CHUNKS], F32)
-                total_sq = const.tile([P, N_CHUNKS], F32)
+                for g in range(GROUPS + 2):
+                    if g < GROUPS and g % NORM_GROUPS == 0:
+                        first_norm(g)
+                    if 1 <= g <= GROUPS:
+                        quantise(g - 1)
+                    if g < GROUPS:
+                        regroup(g)
+                    if 1 <= g <= GROUPS:
+                        multiply(g - 1)
+                    if g >= 2:
+                        hidden_statistics(g - 2)
+
+                mean_var1 = const.tile([P, N_CHUNKS, 2], F32)
+                total = const.tile([P, SUM_CHUNKS], F32)
+                total_sq = const.tile([P, SUM_CHUNKS], F32)
+                mean_sq = const.tile([P, SUM_CHUNKS], F32)
                 nc.vector.tensor_reduce(out=total[:], in_=relu_sums[:], axis=mybir.AxisListType.X, op=ALU.add)
                 nc.vector.tensor_reduce(out=total_sq[:], in_=square_sums[:], axis=mybir.AxisListType.X, op=ALU.add)
-                nc.vector.memset(stats1[:, :, last], count)
-                nc.vector.tensor_scalar(
-                    out=stats1[:, :, last + 1], in0=total[:], scalar1=1.0 / count, scalar2=None, op0=ALU.mult
+                mean = mean_var1[:, 0:SUM_CHUNKS, 0]
+                nc.vector.tensor_scalar(out=mean, in0=total[:], scalar1=1.0 / ROWS, scalar2=None, op0=ALU.mult)
+                nc.vector.tensor_tensor(out=mean_sq[:], in0=mean, in1=mean, op=ALU.mult)
+                nc.vector.scalar_tensor_tensor(
+                    out=mean_var1[:, 0:SUM_CHUNKS, 1],
+                    in0=total_sq[:],
+                    scalar=1.0 / ROWS,
+                    in1=mean_sq[:],
+                    op0=ALU.mult,
+                    op1=ALU.subtract,
                 )
-                nc.vector.tensor_tensor(out=total[:], in0=total[:], in1=stats1[:, :, last + 1], op=ALU.mult)
-                nc.vector.tensor_tensor(out=stats1[:, :, last + 2], in0=total_sq[:], in1=total[:], op=ALU.subtract)
-                mean_var1 = const.tile([P, N_CHUNKS, 2], F32)
-                for c in range(N_CHUNKS):
-                    nc.vector.bn_aggr(out=mean_var1[:, c, :], in_=stats1[:, c, :])
+                for c in range(SUM_CHUNKS, N_CHUNKS):
+                    nc.vector.bn_aggr(
+                        out=mean_var1[:, c, :], in_=stats1[:, c - SUM_CHUNKS, :, :].rearrange("p a b -> p (a b)")
+                    )
                 scale1, shift1 = norm_coefficients(nc, const, mean_var1, vectors[:, 3, :], vectors[:, 4, :], "1")
 
-        with tc.tile_pool(name="stage", bufs=4) as stage, tc.psum_pool(name="psumC", bufs=6) as psum_c:
-            for g in range(GROUPS):
+        with tc.tile_pool(name="stage", bufs=4) as stage, tc.psum_pool(name="psumC", bufs=8) as psum_c:
+
+            def second_norm(g):
                 cols = slice(g * GROUP, (g + 1) * GROUP)
                 for c in range(N_CHUNKS):
                     nc.vector.tensor_scalar(
@@ -219,6 +248,11 @@ def tile_settransform_pa_kernel(tc, set_feats, g0, b0, W0_words, W0_scales, c0, 
                         op0=ALU.mult,
                         op1=ALU.add,
                     )
+
+            second_norm(0)
+            for g in range(GROUPS):
+                if g + 1 < GROUPS:
+                    second_norm(g + 1)
                 result = stage.tile([P, GROUP_TILES, N_OUT], F32, name="result")
                 for i in range(GROUP_TILES):
                     j = g * GROUP_TILES + i

@@ -23,7 +23,7 @@ N_CHUNKS = N_OUT // P
 ROW_TILES = ROWS // P
 EPS = 1e-5
 
-LOAD_TILES = 8
+LOAD_TILES = 4
 BANK_TILES = 2
 BANK_ROWS = BANK_TILES * P
 STAT_ROWS = 512
@@ -78,7 +78,7 @@ def tile_settransform_pa_kernel(tc, set_feats, g0, b0, W0_words, W0_scales, c0, 
             xT = xT_pool.tile([P, PACK, ROWS], BF16)
 
             stats0 = const.tile([P, PACK, ROWS // STAT_ROWS, STAT_WIDTH], F32)
-            with tc.tile_pool(name="load", bufs=4) as load, tc.psum_pool(name="psumA", bufs=4) as psum_a:
+            with tc.tile_pool(name="load", bufs=6) as load, tc.psum_pool(name="psumA", bufs=4) as psum_a:
                 for first in range(0, ROW_TILES, LOAD_TILES):
                     x_sb = load.tile([P, LOAD_TILES, K], BF16, name="x_sb")
                     nc.sync.dma_start(out=x_sb[:], in_=x_rows[:, first : first + LOAD_TILES, :])
@@ -132,8 +132,8 @@ def tile_settransform_pa_kernel(tc, set_feats, g0, b0, W0_words, W0_scales, c0, 
                 grouped_of = {}
                 codes_of = {}
 
-                def first_norm(g):
-                    cols = slice(g * GROUP, (g + NORM_GROUPS) * GROUP)
+                def first_norm(g, groups):
+                    cols = slice(g * GROUP, min(g + groups, GROUPS) * GROUP)
                     for t in range(PACK):
                         nc.vector.tensor_scalar(
                             out=xT[:, t, cols],
@@ -200,11 +200,12 @@ def tile_settransform_pa_kernel(tc, set_feats, g0, b0, W0_words, W0_scales, c0, 
                                 accum_out=square_sums[:, c, g // SQUARE_SPAN : g // SQUARE_SPAN + 1],
                             )
 
+                first_norm(0, 1)
                 for g in range(GROUPS + 2):
-                    if g < GROUPS and g % NORM_GROUPS == 0:
-                        first_norm(g)
                     if 1 <= g <= GROUPS:
                         quantise(g - 1)
+                    if g < GROUPS and g % NORM_GROUPS == 1:
+                        first_norm(g, NORM_GROUPS)
                     if g < GROUPS:
                         regroup(g)
                     if 1 <= g <= GROUPS:
@@ -213,14 +214,18 @@ def tile_settransform_pa_kernel(tc, set_feats, g0, b0, W0_words, W0_scales, c0, 
                         hidden_statistics(g - 2)
 
                 mean_var1 = const.tile([P, N_CHUNKS, 2], F32)
+                for c in range(SUM_CHUNKS, N_CHUNKS):
+                    nc.vector.bn_aggr(
+                        out=mean_var1[:, c, :], in_=stats1[:, c - SUM_CHUNKS, :, :].rearrange("p a b -> p (a b)")
+                    )
                 total = const.tile([P, SUM_CHUNKS], F32)
                 total_sq = const.tile([P, SUM_CHUNKS], F32)
                 mean_sq = const.tile([P, SUM_CHUNKS], F32)
-                nc.vector.tensor_reduce(out=total[:], in_=relu_sums[:], axis=mybir.AxisListType.X, op=ALU.add)
-                nc.vector.tensor_reduce(out=total_sq[:], in_=square_sums[:], axis=mybir.AxisListType.X, op=ALU.add)
                 mean = mean_var1[:, 0:SUM_CHUNKS, 0]
+                nc.vector.tensor_reduce(out=total[:], in_=relu_sums[:], axis=mybir.AxisListType.X, op=ALU.add)
                 nc.vector.tensor_scalar(out=mean, in0=total[:], scalar1=1.0 / ROWS, scalar2=None, op0=ALU.mult)
                 nc.vector.tensor_tensor(out=mean_sq[:], in0=mean, in1=mean, op=ALU.mult)
+                nc.vector.tensor_reduce(out=total_sq[:], in_=square_sums[:], axis=mybir.AxisListType.X, op=ALU.add)
                 nc.vector.scalar_tensor_tensor(
                     out=mean_var1[:, 0:SUM_CHUNKS, 1],
                     in0=total_sq[:],
@@ -229,10 +234,6 @@ def tile_settransform_pa_kernel(tc, set_feats, g0, b0, W0_words, W0_scales, c0, 
                     op0=ALU.mult,
                     op1=ALU.subtract,
                 )
-                for c in range(SUM_CHUNKS, N_CHUNKS):
-                    nc.vector.bn_aggr(
-                        out=mean_var1[:, c, :], in_=stats1[:, c - SUM_CHUNKS, :, :].rearrange("p a b -> p (a b)")
-                    )
                 scale1, shift1 = norm_coefficients(nc, const, mean_var1, vectors[:, 3, :], vectors[:, 4, :], "1")
 
         with tc.tile_pool(name="stage", bufs=4) as stage, tc.psum_pool(name="psumC", bufs=8) as psum_c:

@@ -24,6 +24,10 @@ ROW_TILES = ROWS // P
 EPS = 1e-5
 
 LOAD_TILES = 4
+FIRST_LOADS = (1, 1, 2)
+PE_PLANE = 3
+STAT_MARKS = tuple(range(512, 7681, 512)) + (7936, 8192)
+SQUARE_MARKS = tuple(range(1024, 7169, 1024)) + (7936, 8192)
 BANK_TILES = 2
 BANK_ROWS = BANK_TILES * P
 STAT_ROWS = 512
@@ -39,6 +43,7 @@ SUM_CHUNKS = 2
 SQUARE_SPAN = 2
 
 VECTOR_EVERY = 4
+STORE_TILES = (1, 1, 2) + (4,) * 15
 
 
 def norm_coefficients(nc, pool, mean_var, gain, shift_in, label):
@@ -64,6 +69,10 @@ def tile_settransform_pa_kernel(tc, set_feats, g0, b0, W0_words, W0_scales, c0, 
         identity = const.tile([P, P], F32)
         make_identity(nc, identity[:])
 
+        identity_bf = const.tile([P, P], BF16)
+        make_identity(nc, identity_bf[:])
+        ones = const.tile([P, 1], BF16)
+        nc.vector.memset(ones[:], 1.0)
         warm = const.tile([P, 1], F32)
         nc.vector.memset(warm[:], 1.0)
         nc.scalar.sqrt(out=warm[:], in_=warm[:])
@@ -77,30 +86,56 @@ def tile_settransform_pa_kernel(tc, set_feats, g0, b0, W0_words, W0_scales, c0, 
         with tc.tile_pool(name="xT", bufs=1) as xT_pool:
             xT = xT_pool.tile([P, PACK, ROWS], BF16)
 
-            stats0 = const.tile([P, PACK, ROWS // STAT_ROWS, STAT_WIDTH], F32)
-            with tc.tile_pool(name="load", bufs=6) as load, tc.psum_pool(name="psumA", bufs=4) as psum_a:
-                for first in range(0, ROW_TILES, LOAD_TILES):
+            stats0 = const.tile([P, PACK, len(STAT_MARKS), STAT_WIDTH], F32)
+            squares0 = const.tile([P, len(SQUARE_MARKS)], F32)
+            with tc.tile_pool(name="load", bufs=6) as load, tc.psum_pool(name="psumA", bufs=6) as psum_a, tc.psum_pool(
+                name="psumS", bufs=1
+            ) as psum_s:
+                column_sum = psum_s.tile([P, 1], F32)
+                unread0 = load.tile([P, 1024], F32, name="unread0", bufs=1)
+                sizes = list(FIRST_LOADS) + [LOAD_TILES] * ((ROW_TILES - sum(FIRST_LOADS)) // LOAD_TILES)
+                j = 0
+                flipped = None
+                stat_from = 0
+                square_from = 0
+                for size in sizes:
                     x_sb = load.tile([P, LOAD_TILES, K], BF16, name="x_sb")
-                    nc.sync.dma_start(out=x_sb[:], in_=x_rows[:, first : first + LOAD_TILES, :])
-                    for pair in range(0, LOAD_TILES, BANK_TILES):
-                        start_row = (first + pair) * P
-                        flipped = psum_a.tile([P, WORDS, BANK_ROWS], F32, name="flipped")
-                        for u in range(WORDS):
-                            for i in range(BANK_TILES):
-                                words = x_sb[:, pair + i, :].bitcast(F32)
-                                nc.tensor.transpose(
-                                    flipped[:, u, i * P : (i + 1) * P], words[:, u : K // HALVES : WORDS], identity[:]
-                                )
-                        nc.scalar.copy(
-                            out=xT[:, :, start_row : start_row + BANK_ROWS].rearrange("p (u e) r -> p u e r", e=HALVES),
-                            in_=flipped[:].bitcast(BF16).rearrange("p u (r e) -> p u e r", e=HALVES),
+                    nc.sync.dma_start(out=x_sb[:, 0:size, :], in_=x_rows[:, j : j + size, :])
+                    for i in range(size):
+                        half = j % BANK_TILES
+                        if half == 0:
+                            flipped = psum_a.tile([P, PACK, BANK_ROWS], BF16, name="flipped")
+                        for t in range(PACK):
+                            nc.tensor.transpose(
+                                flipped[:, t, half * P : (half + 1) * P], x_sb[:, i, t:K:PACK], identity_bf[:]
+                            )
+                        nc.tensor.matmul(
+                            out=column_sum[:],
+                            lhsT=x_sb[:, i, PE_PLANE:K:PACK],
+                            rhs=ones[:],
+                            start=(j == 0),
+                            stop=(j == ROW_TILES - 1),
                         )
-                        if (start_row + BANK_ROWS) % STAT_ROWS == 0:
-                            piece = start_row // STAT_ROWS
+                        j += 1
+                        rows_done = j * P
+                        if half == BANK_TILES - 1:
+                            nc.scalar.copy(out=xT[:, :, rows_done - BANK_ROWS : rows_done], in_=flipped[:])
+                        if rows_done in STAT_MARKS:
                             for t in range(PACK):
-                                nc.vector.bn_stats(
-                                    out=stats0[:, t, piece, :], in_=xT[:, t, piece * STAT_ROWS : (piece + 1) * STAT_ROWS]
-                                )
+                                if t != PE_PLANE:
+                                    nc.vector.bn_stats(
+                                        out=stats0[:, t, STAT_MARKS.index(rows_done), :], in_=xT[:, t, stat_from:rows_done]
+                                    )
+                            stat_from = rows_done
+                        if rows_done in SQUARE_MARKS:
+                            slot0 = SQUARE_MARKS.index(rows_done)
+                            nc.scalar.activation(
+                                out=unread0[:, 0 : rows_done - square_from],
+                                in_=xT[:, PE_PLANE, square_from:rows_done],
+                                func=ACT.Square,
+                                accum_out=squares0[:, slot0 : slot0 + 1],
+                            )
+                            square_from = rows_done
 
                 nc.sync.dma_start(
                     out=w_words[:].bitcast(I32), in_=W0_words[0].rearrange("p n t -> p (n t)").bitcast(I32)
@@ -122,7 +157,22 @@ def tile_settransform_pa_kernel(tc, set_feats, g0, b0, W0_words, W0_scales, c0, 
 
                 mean_var0 = const.tile([P, PACK, 2], F32)
                 for t in range(PACK):
-                    nc.vector.bn_aggr(out=mean_var0[:, t, :], in_=stats0[:, t, :, :].rearrange("p a b -> p (a b)"))
+                    if t != PE_PLANE:
+                        nc.vector.bn_aggr(out=mean_var0[:, t, :], in_=stats0[:, t, :, :].rearrange("p a b -> p (a b)"))
+                total_sq0 = const.tile([P, 1], F32)
+                mean_sq0 = const.tile([P, 1], F32)
+                mean0 = mean_var0[:, PE_PLANE, 0:1]
+                nc.vector.tensor_scalar(out=mean0, in0=column_sum[:], scalar1=1.0 / ROWS, scalar2=None, op0=ALU.mult)
+                nc.vector.tensor_tensor(out=mean_sq0[:], in0=mean0, in1=mean0, op=ALU.mult)
+                nc.vector.tensor_reduce(out=total_sq0[:], in_=squares0[:], axis=mybir.AxisListType.X, op=ALU.add)
+                nc.vector.scalar_tensor_tensor(
+                    out=mean_var0[:, PE_PLANE, 1:2],
+                    in0=total_sq0[:],
+                    scalar=1.0 / ROWS,
+                    in1=mean_sq0[:],
+                    op0=ALU.mult,
+                    op1=ALU.subtract,
+                )
                 scale0, shift0 = norm_coefficients(nc, const, mean_var0, vectors[:, 0, :], vectors[:, 1, :], "0")
 
             relu_sums = const.tile([P, SUM_CHUNKS, GROUPS], F32)
@@ -238,8 +288,8 @@ def tile_settransform_pa_kernel(tc, set_feats, g0, b0, W0_words, W0_scales, c0, 
 
         with tc.tile_pool(name="stage", bufs=4) as stage, tc.psum_pool(name="psumC", bufs=8) as psum_c:
 
-            def second_norm(g):
-                cols = slice(g * GROUP, (g + 1) * GROUP)
+            def second_norm(first_tile, tiles):
+                cols = slice(first_tile * P, (first_tile + tiles) * P)
                 for c in range(N_CHUNKS):
                     nc.vector.tensor_scalar(
                         out=h0T[:, c, cols],
@@ -250,18 +300,21 @@ def tile_settransform_pa_kernel(tc, set_feats, g0, b0, W0_words, W0_scales, c0, 
                         op1=ALU.add,
                     )
 
-            second_norm(0)
-            for g in range(GROUPS):
-                if g + 1 < GROUPS:
-                    second_norm(g + 1)
+            firsts = [sum(STORE_TILES[0:s]) for s in range(len(STORE_TILES))]
+            second_norm(firsts[0], STORE_TILES[0])
+            for s in range(len(STORE_TILES)):
+                if s + 1 < len(STORE_TILES):
+                    second_norm(firsts[s + 1], STORE_TILES[s + 1])
                 result = stage.tile([P, GROUP_TILES, N_OUT], F32, name="result")
-                for i in range(GROUP_TILES):
-                    j = g * GROUP_TILES + i
+                for i in range(STORE_TILES[s]):
+                    j = firsts[s] + i
                     back = psum_c.tile([P, N_OUT], F32, name="back")
                     for c in range(N_CHUNKS):
                         nc.tensor.transpose(back[:, c * P : (c + 1) * P], h0T[:, c, j * P : (j + 1) * P], identity[:])
-                    if j % VECTOR_EVERY == 0:
+                    if j % VECTOR_EVERY == VECTOR_EVERY - 1:
                         nc.vector.tensor_copy(out=result[:, i, :], in_=back[:])
                     else:
                         nc.scalar.copy(out=result[:, i, :], in_=back[:])
-                nc.sync.dma_start(out=out_rows[:, g * GROUP_TILES : (g + 1) * GROUP_TILES, :], in_=result[:])
+                nc.sync.dma_start(
+                    out=out_rows[:, firsts[s] : firsts[s] + STORE_TILES[s], :], in_=result[:, 0 : STORE_TILES[s], :]
+                )

@@ -26,6 +26,7 @@ EPS = 1e-5
 LOAD_TILES = 4
 FIRST_LOADS = (1, 1, 2)
 PE_PLANE = 3
+WARM_MATMULS = 25
 STAT_MARKS = tuple(range(512, 7681, 512)) + (7936, 8192)
 SQUARE_MARKS = tuple(range(1024, 7169, 1024)) + (7936, 8192)
 BANK_TILES = 2
@@ -90,8 +91,9 @@ def tile_settransform_pa_kernel(tc, set_feats, g0, b0, W0_words, W0_scales, c0, 
             squares0 = const.tile([P, len(SQUARE_MARKS)], F32)
             with tc.tile_pool(name="load", bufs=6) as load, tc.psum_pool(name="psumA", bufs=6) as psum_a, tc.psum_pool(
                 name="psumS", bufs=1
-            ) as psum_s:
+            ) as psum_s, tc.psum_pool(name="psumW", bufs=1) as psum_w:
                 column_sum = psum_s.tile([P, 1], F32)
+                unread_bank = psum_w.tile([P, K], F32)
                 unread0 = load.tile([P, 1024], F32, name="unread0", bufs=1)
                 sizes = list(FIRST_LOADS) + [LOAD_TILES] * ((ROW_TILES - sum(FIRST_LOADS)) // LOAD_TILES)
                 j = 0
@@ -116,6 +118,10 @@ def tile_settransform_pa_kernel(tc, set_feats, g0, b0, W0_words, W0_scales, c0, 
                             start=(j == 0),
                             stop=(j == ROW_TILES - 1),
                         )
+                        if (j * WARM_MATMULS) // ROW_TILES != ((j + 1) * WARM_MATMULS) // ROW_TILES:
+                            nc.tensor.matmul(
+                                out=unread_bank[:], lhsT=identity_bf[:], rhs=x_sb[:, i, :], start=True, stop=True
+                            )
                         j += 1
                         rows_done = j * P
                         if half == BANK_TILES - 1:

@@ -66,7 +66,7 @@ def tile_settransform_pa_kernel(tc, set_feats, g0, b0, W0_words, W0_scales, c0, 
     x_rows = set_feats.rearrange("b s k -> (b s) k").rearrange("(p j) k -> p j k", j=ROW_TILES)
     out_rows = out.rearrange("b s n -> (b s) n").rearrange("(p j) n -> p j n", j=ROW_TILES)
 
-    with tc.manual_schedule(), tc.tile_pool(name="const", bufs=1) as const, tc.tile_pool(name="hidden", bufs=1) as hidden:
+    with tc.manual_schedule(), tc.tile_pool(name="const", bufs=1) as const:
         identity = const.tile([P, P], F32)
         make_identity(nc, identity[:])
 
@@ -82,14 +82,12 @@ def tile_settransform_pa_kernel(tc, set_feats, g0, b0, W0_words, W0_scales, c0, 
         w_plane = const.tile([P, N_OUT], U8, align_bytes=64)
         nc.vector.memset(w_plane[:].bitcast(I32), 0)
 
-        h0T = hidden.tile([P, N_CHUNKS, ROWS], F32)
-
         with tc.tile_pool(name="xT", bufs=1) as xT_pool:
             xT = xT_pool.tile([P, PACK, ROWS], BF16)
 
             stats0 = const.tile([P, PACK, len(STAT_MARKS), STAT_WIDTH], F32)
             squares0 = const.tile([P, len(SQUARE_MARKS)], F32)
-            with tc.tile_pool(name="load", bufs=6) as load, tc.psum_pool(name="psumA", bufs=6) as psum_a, tc.psum_pool(
+            with tc.tile_pool(name="load", bufs=18) as load, tc.psum_pool(name="psumA", bufs=6) as psum_a, tc.psum_pool(
                 name="psumS", bufs=1
             ) as psum_s, tc.psum_pool(name="psumW", bufs=1) as psum_w:
                 column_sum = psum_s.tile([P, 1], F32)
@@ -181,146 +179,149 @@ def tile_settransform_pa_kernel(tc, set_feats, g0, b0, W0_words, W0_scales, c0, 
                 )
                 scale0, shift0 = norm_coefficients(nc, const, mean_var0, vectors[:, 0, :], vectors[:, 1, :], "0")
 
-            relu_sums = const.tile([P, SUM_CHUNKS, GROUPS], F32)
-            square_sums = const.tile([P, SUM_CHUNKS, GROUPS // SQUARE_SPAN], F32)
-            stats1 = const.tile([P, N_CHUNKS - SUM_CHUNKS, GROUPS, STAT_WIDTH], F32)
-            with tc.tile_pool(name="work", bufs=2) as work, tc.psum_pool(name="psumB", bufs=8) as psum_b:
-                grouped_of = {}
-                codes_of = {}
+            with tc.tile_pool(name="hidden", bufs=1) as hidden:
+                h0T = hidden.tile([P, N_CHUNKS, ROWS], F32)
 
-                def first_norm(g, groups):
-                    cols = slice(g * GROUP, min(g + groups, GROUPS) * GROUP)
-                    for t in range(PACK):
-                        nc.vector.tensor_scalar(
-                            out=xT[:, t, cols],
-                            in0=xT[:, t, cols],
-                            scalar1=scale0[:, t : t + 1],
-                            scalar2=shift0[:, t : t + 1],
-                            op0=ALU.mult,
-                            op1=ALU.add,
-                        )
+                relu_sums = const.tile([P, SUM_CHUNKS, GROUPS], F32)
+                square_sums = const.tile([P, SUM_CHUNKS, GROUPS // SQUARE_SPAN], F32)
+                stats1 = const.tile([P, N_CHUNKS - SUM_CHUNKS, GROUPS, STAT_WIDTH], F32)
+                with tc.tile_pool(name="work", bufs=2) as work, tc.psum_pool(name="psumB", bufs=8) as psum_b:
+                    grouped_of = {}
+                    codes_of = {}
 
-                def regroup(g):
-                    grouped = work.tile([P, GROUP, PACK], BF16, name="grouped", align_bytes=64)
-                    nc.vector.tensor_copy(
-                        out=grouped[:].rearrange("p (c i) t -> p c t i", i=RUN),
-                        in_=xT[:, :, g * GROUP : (g + 1) * GROUP].rearrange("p t (c i) -> p c t i", i=RUN),
-                    )
-                    grouped_of[g] = grouped
-
-                def quantise(g):
-                    codes = work.tile([P, GROUP], U32, name="codes", align_bytes=64)
-                    x_plane = work.tile([P, GROUP], U8, name="x_plane", align_bytes=64)
-                    nc.vector.quantize_mx(
-                        out=codes[:].bitcast(FP8X4),
-                        scales=x_plane[:],
-                        in_=grouped_of[g][:].rearrange("p r t -> p (r t)"),
-                    )
-                    codes_of[g] = (codes, x_plane)
-
-                def multiply(g):
-                    codes, x_plane = codes_of[g]
-                    for c in range(N_CHUNKS):
-                        n_cols = slice(c * P, (c + 1) * P)
-                        acc = psum_b.tile([P, GROUP], F32, name="acc")
-                        nc.tensor.matmul_mx(
-                            out=acc[:],
-                            lhsT=w_words[:, n_cols].bitcast(FP8X4),
-                            lhsT_scale=w_plane[:, n_cols],
-                            rhs=codes[:].bitcast(FP8X4),
-                            rhs_scale=x_plane[:],
-                            start=True,
-                            stop=True,
-                        )
-                        nc.scalar.activation(
-                            out=h0T[:, c, g * GROUP : (g + 1) * GROUP],
-                            in_=acc[:],
-                            func=ACT.Relu,
-                            bias=vectors[:, 2, c : c + 1],
-                            scale=1.0,
-                            accum_out=relu_sums[:, c, g : g + 1] if c < SUM_CHUNKS else None,
-                        )
-
-                def hidden_statistics(g):
-                    for c in range(SUM_CHUNKS, N_CHUNKS):
-                        nc.vector.bn_stats(
-                            out=stats1[:, c - SUM_CHUNKS, g, :], in_=h0T[:, c, g * GROUP : (g + 1) * GROUP]
-                        )
-                    if g % SQUARE_SPAN == SQUARE_SPAN - 1:
-                        for c in range(SUM_CHUNKS):
-                            unread = work.tile([P, SQUARE_SPAN * GROUP], BF16, name="unread")
-                            nc.scalar.activation(
-                                out=unread[:],
-                                in_=h0T[:, c, (g + 1 - SQUARE_SPAN) * GROUP : (g + 1) * GROUP],
-                                func=ACT.Square,
-                                accum_out=square_sums[:, c, g // SQUARE_SPAN : g // SQUARE_SPAN + 1],
+                    def first_norm(g, groups):
+                        cols = slice(g * GROUP, min(g + groups, GROUPS) * GROUP)
+                        for t in range(PACK):
+                            nc.vector.tensor_scalar(
+                                out=xT[:, t, cols],
+                                in0=xT[:, t, cols],
+                                scalar1=scale0[:, t : t + 1],
+                                scalar2=shift0[:, t : t + 1],
+                                op0=ALU.mult,
+                                op1=ALU.add,
                             )
 
-                first_norm(0, 1)
-                for g in range(GROUPS + 2):
-                    if 1 <= g <= GROUPS:
-                        quantise(g - 1)
-                    if g < GROUPS and g % NORM_GROUPS == 1:
-                        first_norm(g, NORM_GROUPS)
-                    if g < GROUPS:
-                        regroup(g)
-                    if 1 <= g <= GROUPS:
-                        multiply(g - 1)
-                    if g >= 2:
-                        hidden_statistics(g - 2)
+                    def regroup(g):
+                        grouped = work.tile([P, GROUP, PACK], BF16, name="grouped", align_bytes=64)
+                        nc.vector.tensor_copy(
+                            out=grouped[:].rearrange("p (c i) t -> p c t i", i=RUN),
+                            in_=xT[:, :, g * GROUP : (g + 1) * GROUP].rearrange("p t (c i) -> p c t i", i=RUN),
+                        )
+                        grouped_of[g] = grouped
 
-                mean_var1 = const.tile([P, N_CHUNKS, 2], F32)
-                for c in range(SUM_CHUNKS, N_CHUNKS):
-                    nc.vector.bn_aggr(
-                        out=mean_var1[:, c, :], in_=stats1[:, c - SUM_CHUNKS, :, :].rearrange("p a b -> p (a b)")
-                    )
-                total = const.tile([P, SUM_CHUNKS], F32)
-                total_sq = const.tile([P, SUM_CHUNKS], F32)
-                mean_sq = const.tile([P, SUM_CHUNKS], F32)
-                mean = mean_var1[:, 0:SUM_CHUNKS, 0]
-                nc.vector.tensor_reduce(out=total[:], in_=relu_sums[:], axis=mybir.AxisListType.X, op=ALU.add)
-                nc.vector.tensor_scalar(out=mean, in0=total[:], scalar1=1.0 / ROWS, scalar2=None, op0=ALU.mult)
-                nc.vector.tensor_tensor(out=mean_sq[:], in0=mean, in1=mean, op=ALU.mult)
-                nc.vector.tensor_reduce(out=total_sq[:], in_=square_sums[:], axis=mybir.AxisListType.X, op=ALU.add)
-                nc.vector.scalar_tensor_tensor(
-                    out=mean_var1[:, 0:SUM_CHUNKS, 1],
-                    in0=total_sq[:],
-                    scalar=1.0 / ROWS,
-                    in1=mean_sq[:],
-                    op0=ALU.mult,
-                    op1=ALU.subtract,
-                )
-                scale1, shift1 = norm_coefficients(nc, const, mean_var1, vectors[:, 3, :], vectors[:, 4, :], "1")
+                    def quantise(g):
+                        codes = work.tile([P, GROUP], U32, name="codes", align_bytes=64)
+                        x_plane = work.tile([P, GROUP], U8, name="x_plane", align_bytes=64)
+                        nc.vector.quantize_mx(
+                            out=codes[:].bitcast(FP8X4),
+                            scales=x_plane[:],
+                            in_=grouped_of[g][:].rearrange("p r t -> p (r t)"),
+                        )
+                        codes_of[g] = (codes, x_plane)
 
-        with tc.tile_pool(name="stage", bufs=4) as stage, tc.psum_pool(name="psumC", bufs=8) as psum_c:
+                    def multiply(g):
+                        codes, x_plane = codes_of[g]
+                        for c in range(N_CHUNKS):
+                            n_cols = slice(c * P, (c + 1) * P)
+                            acc = psum_b.tile([P, GROUP], F32, name="acc")
+                            nc.tensor.matmul_mx(
+                                out=acc[:],
+                                lhsT=w_words[:, n_cols].bitcast(FP8X4),
+                                lhsT_scale=w_plane[:, n_cols],
+                                rhs=codes[:].bitcast(FP8X4),
+                                rhs_scale=x_plane[:],
+                                start=True,
+                                stop=True,
+                            )
+                            nc.scalar.activation(
+                                out=h0T[:, c, g * GROUP : (g + 1) * GROUP],
+                                in_=acc[:],
+                                func=ACT.Relu,
+                                bias=vectors[:, 2, c : c + 1],
+                                scale=1.0,
+                                accum_out=relu_sums[:, c, g : g + 1] if c < SUM_CHUNKS else None,
+                            )
 
-            def second_norm(first_tile, tiles):
-                cols = slice(first_tile * P, (first_tile + tiles) * P)
-                for c in range(N_CHUNKS):
-                    nc.vector.tensor_scalar(
-                        out=h0T[:, c, cols],
-                        in0=h0T[:, c, cols],
-                        scalar1=scale1[:, c : c + 1],
-                        scalar2=shift1[:, c : c + 1],
+                    def hidden_statistics(g):
+                        for c in range(SUM_CHUNKS, N_CHUNKS):
+                            nc.vector.bn_stats(
+                                out=stats1[:, c - SUM_CHUNKS, g, :], in_=h0T[:, c, g * GROUP : (g + 1) * GROUP]
+                            )
+                        if g % SQUARE_SPAN == SQUARE_SPAN - 1:
+                            for c in range(SUM_CHUNKS):
+                                unread = work.tile([P, SQUARE_SPAN * GROUP], BF16, name="unread")
+                                nc.scalar.activation(
+                                    out=unread[:],
+                                    in_=h0T[:, c, (g + 1 - SQUARE_SPAN) * GROUP : (g + 1) * GROUP],
+                                    func=ACT.Square,
+                                    accum_out=square_sums[:, c, g // SQUARE_SPAN : g // SQUARE_SPAN + 1],
+                                )
+
+                    first_norm(0, 1)
+                    for g in range(GROUPS + 2):
+                        if 1 <= g <= GROUPS:
+                            quantise(g - 1)
+                        if g < GROUPS and g % NORM_GROUPS == 1:
+                            first_norm(g, NORM_GROUPS)
+                        if g < GROUPS:
+                            regroup(g)
+                        if 1 <= g <= GROUPS:
+                            multiply(g - 1)
+                        if g >= 2:
+                            hidden_statistics(g - 2)
+
+                    mean_var1 = const.tile([P, N_CHUNKS, 2], F32)
+                    for c in range(SUM_CHUNKS, N_CHUNKS):
+                        nc.vector.bn_aggr(
+                            out=mean_var1[:, c, :], in_=stats1[:, c - SUM_CHUNKS, :, :].rearrange("p a b -> p (a b)")
+                        )
+                    total = const.tile([P, SUM_CHUNKS], F32)
+                    total_sq = const.tile([P, SUM_CHUNKS], F32)
+                    mean_sq = const.tile([P, SUM_CHUNKS], F32)
+                    mean = mean_var1[:, 0:SUM_CHUNKS, 0]
+                    nc.vector.tensor_reduce(out=total[:], in_=relu_sums[:], axis=mybir.AxisListType.X, op=ALU.add)
+                    nc.vector.tensor_scalar(out=mean, in0=total[:], scalar1=1.0 / ROWS, scalar2=None, op0=ALU.mult)
+                    nc.vector.tensor_tensor(out=mean_sq[:], in0=mean, in1=mean, op=ALU.mult)
+                    nc.vector.tensor_reduce(out=total_sq[:], in_=square_sums[:], axis=mybir.AxisListType.X, op=ALU.add)
+                    nc.vector.scalar_tensor_tensor(
+                        out=mean_var1[:, 0:SUM_CHUNKS, 1],
+                        in0=total_sq[:],
+                        scalar=1.0 / ROWS,
+                        in1=mean_sq[:],
                         op0=ALU.mult,
-                        op1=ALU.add,
+                        op1=ALU.subtract,
                     )
+                    scale1, shift1 = norm_coefficients(nc, const, mean_var1, vectors[:, 3, :], vectors[:, 4, :], "1")
 
-            firsts = [sum(STORE_TILES[0:s]) for s in range(len(STORE_TILES))]
-            second_norm(firsts[0], STORE_TILES[0])
-            for s in range(len(STORE_TILES)):
-                if s + 1 < len(STORE_TILES):
-                    second_norm(firsts[s + 1], STORE_TILES[s + 1])
-                result = stage.tile([P, GROUP_TILES, N_OUT], F32, name="result")
-                for i in range(STORE_TILES[s]):
-                    j = firsts[s] + i
-                    back = psum_c.tile([P, N_OUT], F32, name="back")
-                    for c in range(N_CHUNKS):
-                        nc.tensor.transpose(back[:, c * P : (c + 1) * P], h0T[:, c, j * P : (j + 1) * P], identity[:])
-                    if j % VECTOR_EVERY == VECTOR_EVERY - 1:
-                        nc.vector.tensor_copy(out=result[:, i, :], in_=back[:])
-                    else:
-                        nc.scalar.copy(out=result[:, i, :], in_=back[:])
-                nc.sync.dma_start(
-                    out=out_rows[:, firsts[s] : firsts[s] + STORE_TILES[s], :], in_=result[:, 0 : STORE_TILES[s], :]
-                )
+                with tc.tile_pool(name="stage", bufs=4) as stage, tc.psum_pool(name="psumC", bufs=8) as psum_c:
+
+                    def second_norm(first_tile, tiles):
+                        cols = slice(first_tile * P, (first_tile + tiles) * P)
+                        for c in range(N_CHUNKS):
+                            nc.vector.tensor_scalar(
+                                out=h0T[:, c, cols],
+                                in0=h0T[:, c, cols],
+                                scalar1=scale1[:, c : c + 1],
+                                scalar2=shift1[:, c : c + 1],
+                                op0=ALU.mult,
+                                op1=ALU.add,
+                            )
+
+                    firsts = [sum(STORE_TILES[0:s]) for s in range(len(STORE_TILES))]
+                    second_norm(firsts[0], STORE_TILES[0])
+                    for s in range(len(STORE_TILES)):
+                        if s + 1 < len(STORE_TILES):
+                            second_norm(firsts[s + 1], STORE_TILES[s + 1])
+                        result = stage.tile([P, GROUP_TILES, N_OUT], F32, name="result")
+                        for i in range(STORE_TILES[s]):
+                            j = firsts[s] + i
+                            back = psum_c.tile([P, N_OUT], F32, name="back")
+                            for c in range(N_CHUNKS):
+                                nc.tensor.transpose(back[:, c * P : (c + 1) * P], h0T[:, c, j * P : (j + 1) * P], identity[:])
+                            if j % VECTOR_EVERY == VECTOR_EVERY - 1:
+                                nc.vector.tensor_copy(out=result[:, i, :], in_=back[:])
+                            else:
+                                nc.scalar.copy(out=result[:, i, :], in_=back[:])
+                        nc.sync.dma_start(
+                            out=out_rows[:, firsts[s] : firsts[s] + STORE_TILES[s], :], in_=result[:, 0 : STORE_TILES[s], :]
+                        )

@@ -47,14 +47,12 @@ VECTOR_EVERY = 4
 STORE_TILES = (1, 1, 2) + (4,) * 15
 
 
-def norm_coefficients(nc, pool, mean_var, gain, shift_in, label):
+def norm_coefficients(nc, pool, eps, mean_var, gain, shift_in, label):
     width = gain.shape[1]
     rstd = pool.tile([P, width], F32, name="rstd" + label)
     scale = pool.tile([P, width], F32, name="scale" + label)
     shift = pool.tile([P, width], F32, name="shift" + label)
-    nc.vector.tensor_scalar(out=rstd[:], in0=mean_var[:, :, 1], scalar1=EPS, scalar2=None, op0=ALU.add)
-    nc.scalar.sqrt(out=rstd[:], in_=rstd[:])
-    nc.vector.reciprocal(out=rstd[:], in_=rstd[:])
+    nc.scalar.activation(out=rstd[:], in_=mean_var[:, :, 1], func=ACT.Abs_reciprocal_sqrt, bias=eps[:], scale=1.0)
     nc.vector.tensor_tensor(out=scale[:], in0=rstd[:], in1=gain, op=ALU.mult)
     nc.vector.tensor_tensor(out=shift[:], in0=mean_var[:, :, 0], in1=scale[:], op=ALU.mult)
     nc.vector.tensor_tensor(out=shift[:], in0=shift_in, in1=shift[:], op=ALU.subtract)
@@ -76,7 +74,9 @@ def tile_settransform_pa_kernel(tc, set_feats, g0, b0, W0_words, W0_scales, c0, 
         nc.vector.memset(ones[:], 1.0)
         warm = const.tile([P, 1], F32)
         nc.vector.memset(warm[:], 1.0)
-        nc.scalar.sqrt(out=warm[:], in_=warm[:])
+        nc.scalar.activation(out=warm[:], in_=warm[:], func=ACT.Abs_reciprocal_sqrt)
+        eps = const.tile([P, 1], F32)
+        nc.vector.memset(eps[:], EPS)
 
         w_words = const.tile([P, N_OUT], U32, align_bytes=64)
         w_plane = const.tile([P, N_OUT], U8, align_bytes=64)
@@ -177,7 +177,7 @@ def tile_settransform_pa_kernel(tc, set_feats, g0, b0, W0_words, W0_scales, c0, 
                     op0=ALU.mult,
                     op1=ALU.subtract,
                 )
-                scale0, shift0 = norm_coefficients(nc, const, mean_var0, vectors[:, 0, :], vectors[:, 1, :], "0")
+                scale0, shift0 = norm_coefficients(nc, const, eps, mean_var0, vectors[:, 0, :], vectors[:, 1, :], "0")
 
             with tc.tile_pool(name="hidden", bufs=1) as hidden:
                 h0T = hidden.tile([P, N_CHUNKS, ROWS], F32)
@@ -291,7 +291,7 @@ def tile_settransform_pa_kernel(tc, set_feats, g0, b0, W0_words, W0_scales, c0, 
                         op0=ALU.mult,
                         op1=ALU.subtract,
                     )
-                    scale1, shift1 = norm_coefficients(nc, const, mean_var1, vectors[:, 3, :], vectors[:, 4, :], "1")
+                    scale1, shift1 = norm_coefficients(nc, const, eps, mean_var1, vectors[:, 3, :], vectors[:, 4, :], "1")
 
                 with tc.tile_pool(name="stage", bufs=4) as stage, tc.psum_pool(name="psumC", bufs=8) as psum_c:
 

@@ -25,27 +25,26 @@ EPS = 1e-5
 
 LOAD_TILES = 4
 FIRST_LOADS = (1, 1, 2)
-PE_PLANE = 3
-WARM_MATMULS = 25
-STAT_MARKS = tuple(range(512, 7681, 512)) + (7936, 8192)
-SQUARE_MARKS = tuple(range(1024, 7169, 1024)) + (7936, 8192)
-BANK_TILES = 2
-BANK_ROWS = BANK_TILES * P
 STAT_ROWS = 512
+STAT_TILES = STAT_ROWS // P
+STAT_GROUPS = ROWS // STAT_ROWS
 STAT_WIDTH = 6
+SCALAR_WORD = 1
 
 GROUP = 512
 GROUP_TILES = GROUP // P
 GROUPS = ROWS // GROUP
-NORM_GROUPS = 4
 RUN = 4
 
-SUM_CHUNKS = 2
-SQUARE_SPAN = 2
+BN_CHUNK = 3
+SHARED_CHUNK = 2
+SUM_CHUNKS = 3
+VECTOR_GROUPS = (2, 5, 8, 11, 14, 15)
+SPANS = tuple((g, 2) for g in range(0, 14, 2)) + ((14, 1), (15, 1))
+SHARED_SPANS = tuple((g, 2) for g in range(0, 14, 3))
 
 VECTOR_EVERY = 4
 STORE_TILES = (1, 1, 2) + (4,) * 15
-
 
 def norm_coefficients(nc, pool, eps, mean_var, gain, shift_in, label):
     width = gain.shape[1]
@@ -67,7 +66,6 @@ def tile_settransform_pa_kernel(tc, set_feats, g0, b0, W0_words, W0_scales, c0, 
     with tc.manual_schedule(), tc.tile_pool(name="const", bufs=1) as const:
         identity = const.tile([P, P], F32)
         make_identity(nc, identity[:])
-
         identity_bf = const.tile([P, P], BF16)
         make_identity(nc, identity_bf[:])
         ones = const.tile([P, 1], BF16)
@@ -82,65 +80,22 @@ def tile_settransform_pa_kernel(tc, set_feats, g0, b0, W0_words, W0_scales, c0, 
         w_plane = const.tile([P, N_OUT], U8, align_bytes=64)
         nc.vector.memset(w_plane[:].bitcast(I32), 0)
 
-        with tc.tile_pool(name="xT", bufs=1) as xT_pool:
-            xT = xT_pool.tile([P, PACK, ROWS], BF16)
+        with tc.tile_pool(name="x", bufs=1) as x_pool, tc.tile_pool(name="hidden", bufs=1) as hidden:
+            x_sb = x_pool.tile([P, ROW_TILES, K], BF16)
+            h0T = hidden.tile([P, N_CHUNKS, ROWS], F32)
 
-            stats0 = const.tile([P, PACK, len(STAT_MARKS), STAT_WIDTH], F32)
-            squares0 = const.tile([P, len(SQUARE_MARKS)], F32)
-            with tc.tile_pool(name="load", bufs=18) as load, tc.psum_pool(name="psumA", bufs=6) as psum_a, tc.psum_pool(
+            stats0 = const.tile([P, HALVES, STAT_GROUPS, STAT_WIDTH], F32)
+            squares0 = const.tile([P, HALVES, STAT_GROUPS], F32)
+            mean_var0 = const.tile([P, PACK, 2], F32)
+            with tc.psum_pool(name="psumV", bufs=3) as psum_v, tc.psum_pool(name="psumA", bufs=3) as psum_a, tc.psum_pool(
                 name="psumS", bufs=1
-            ) as psum_s, tc.psum_pool(name="psumW", bufs=1) as psum_w:
-                column_sum = psum_s.tile([P, 1], F32)
-                unread_bank = psum_w.tile([P, K], F32)
-                unread0 = load.tile([P, 1024], F32, name="unread0", bufs=1)
+            ) as psum_s, tc.tile_pool(name="junk", bufs=2) as junk:
+                sums = [psum_s.tile([P, 512], F32, name="sum%d" % e) for e in range(HALVES)]
                 sizes = list(FIRST_LOADS) + [LOAD_TILES] * ((ROW_TILES - sum(FIRST_LOADS)) // LOAD_TILES)
                 j = 0
-                flipped = None
-                stat_from = 0
-                square_from = 0
                 for size in sizes:
-                    x_sb = load.tile([P, LOAD_TILES, K], BF16, name="x_sb")
-                    nc.sync.dma_start(out=x_sb[:, 0:size, :], in_=x_rows[:, j : j + size, :])
-                    for i in range(size):
-                        half = j % BANK_TILES
-                        if half == 0:
-                            flipped = psum_a.tile([P, PACK, BANK_ROWS], BF16, name="flipped")
-                        for t in range(PACK):
-                            nc.tensor.transpose(
-                                flipped[:, t, half * P : (half + 1) * P], x_sb[:, i, t:K:PACK], identity_bf[:]
-                            )
-                        nc.tensor.matmul(
-                            out=column_sum[:],
-                            lhsT=x_sb[:, i, PE_PLANE:K:PACK],
-                            rhs=ones[:],
-                            start=(j == 0),
-                            stop=(j == ROW_TILES - 1),
-                        )
-                        if (j * WARM_MATMULS) // ROW_TILES != ((j + 1) * WARM_MATMULS) // ROW_TILES:
-                            nc.tensor.matmul(
-                                out=unread_bank[:], lhsT=identity_bf[:], rhs=x_sb[:, i, :], start=True, stop=True
-                            )
-                        j += 1
-                        rows_done = j * P
-                        if half == BANK_TILES - 1:
-                            nc.scalar.copy(out=xT[:, :, rows_done - BANK_ROWS : rows_done], in_=flipped[:])
-                        if rows_done in STAT_MARKS:
-                            for t in range(PACK):
-                                if t != PE_PLANE:
-                                    nc.vector.bn_stats(
-                                        out=stats0[:, t, STAT_MARKS.index(rows_done), :], in_=xT[:, t, stat_from:rows_done]
-                                    )
-                            stat_from = rows_done
-                        if rows_done in SQUARE_MARKS:
-                            slot0 = SQUARE_MARKS.index(rows_done)
-                            nc.scalar.activation(
-                                out=unread0[:, 0 : rows_done - square_from],
-                                in_=xT[:, PE_PLANE, square_from:rows_done],
-                                func=ACT.Square,
-                                accum_out=squares0[:, slot0 : slot0 + 1],
-                            )
-                            square_from = rows_done
-
+                    nc.sync.dma_start(out=x_sb[:, j : j + size, :], in_=x_rows[:, j : j + size, :])
+                    j += size
                 nc.sync.dma_start(
                     out=w_words[:].bitcast(I32), in_=W0_words[0].rearrange("p n t -> p (n t)").bitcast(I32)
                 )
@@ -157,20 +112,45 @@ def tile_settransform_pa_kernel(tc, set_feats, g0, b0, W0_words, W0_scales, c0, 
                     nc.sync.dma_start(out=vectors_bf[:, 2, 0:N_CHUNKS], in_=c0.rearrange("(c p) -> p c", p=P))
                     nc.sync.dma_start(out=vectors_bf[:, 3, 0:N_CHUNKS], in_=g1.rearrange("(c p) -> p c", p=P))
                     nc.sync.dma_start(out=vectors_bf[:, 4, 0:N_CHUNKS], in_=b1.rearrange("(c p) -> p c", p=P))
-                nc.vector.tensor_copy(out=vectors[:], in_=vectors_bf[:, :, 0:PACK])
 
-                mean_var0 = const.tile([P, PACK, 2], F32)
-                for t in range(PACK):
-                    if t != PE_PLANE:
-                        nc.vector.bn_aggr(out=mean_var0[:, t, :], in_=stats0[:, t, :, :].rearrange("p a b -> p (a b)"))
-                total_sq0 = const.tile([P, 1], F32)
-                mean_sq0 = const.tile([P, 1], F32)
-                mean0 = mean_var0[:, PE_PLANE, 0:1]
-                nc.vector.tensor_scalar(out=mean0, in0=column_sum[:], scalar1=1.0 / ROWS, scalar2=None, op0=ALU.mult)
-                nc.vector.tensor_tensor(out=mean_sq0[:], in0=mean0, in1=mean0, op=ALU.mult)
+                for s in range(STAT_GROUPS):
+                    bank_v = psum_v.tile([P, STAT_ROWS], F32, name="bank_v")
+                    bank_a = psum_a.tile([P, STAT_ROWS], F32, name="bank_a")
+                    for i in range(STAT_TILES):
+                        j = s * STAT_TILES + i
+                        words = x_sb[:, j, :].bitcast(F32)
+                        nc.tensor.transpose(bank_v[:, i * P : (i + 1) * P], words[:, 0 : K // HALVES : WORDS], identity[:])
+                        nc.tensor.transpose(bank_a[:, i * P : (i + 1) * P], words[:, 1 : K // HALVES : WORDS], identity[:])
+                        for e in range(HALVES):
+                            nc.tensor.matmul(
+                                out=sums[e][:, 0:1],
+                                lhsT=x_sb[:, j, HALVES * SCALAR_WORD + e : K : PACK],
+                                rhs=ones[:],
+                                start=(j == 0),
+                                stop=(j == ROW_TILES - 1),
+                            )
+                    halves_v = bank_v[:].bitcast(BF16).rearrange("p (r e) -> p e r", e=HALVES)
+                    halves_a = bank_a[:].bitcast(BF16).rearrange("p (r e) -> p e r", e=HALVES)
+                    for e in range(HALVES):
+                        nc.vector.bn_stats(out=stats0[:, e, s, :], in_=halves_v[:, e, :])
+                        unread0 = junk.tile([P, STAT_ROWS], BF16, name="unread0")
+                        nc.scalar.activation(
+                            out=unread0[:], in_=halves_a[:, e, :], func=ACT.Square, accum_out=squares0[:, e, s : s + 1]
+                        )
+                nc.vector.tensor_copy(out=vectors[:], in_=vectors_bf[:, :, 0:PACK])
+                for e in range(HALVES):
+                    nc.vector.bn_aggr(out=mean_var0[:, e, :], in_=stats0[:, e, :, :].rearrange("p a b -> p (a b)"))
+                total_sq0 = const.tile([P, HALVES], F32)
+                mean_sq0 = const.tile([P, HALVES], F32)
+                mean0 = mean_var0[:, HALVES:PACK, 0]
+                for e in range(HALVES):
+                    nc.vector.tensor_scalar(
+                        out=mean_var0[:, HALVES + e, 0:1], in0=sums[e][:, 0:1], scalar1=1.0 / ROWS, scalar2=None, op0=ALU.mult
+                    )
                 nc.vector.tensor_reduce(out=total_sq0[:], in_=squares0[:], axis=mybir.AxisListType.X, op=ALU.add)
+                nc.vector.tensor_tensor(out=mean_sq0[:], in0=mean0, in1=mean0, op=ALU.mult)
                 nc.vector.scalar_tensor_tensor(
-                    out=mean_var0[:, PE_PLANE, 1:2],
+                    out=mean_var0[:, HALVES:PACK, 1],
                     in0=total_sq0[:],
                     scalar=1.0 / ROWS,
                     in1=mean_sq0[:],
@@ -179,149 +159,180 @@ def tile_settransform_pa_kernel(tc, set_feats, g0, b0, W0_words, W0_scales, c0, 
                 )
                 scale0, shift0 = norm_coefficients(nc, const, eps, mean_var0, vectors[:, 0, :], vectors[:, 1, :], "0")
 
-            with tc.tile_pool(name="hidden", bufs=1) as hidden:
-                h0T = hidden.tile([P, N_CHUNKS, ROWS], F32)
+            relu_sums = const.tile([P, SUM_CHUNKS, GROUPS], F32)
+            square_sums = const.tile([P, SUM_CHUNKS, GROUPS], F32)
+            nc.vector.memset(square_sums[:], 0.0)
+            stats1 = const.tile([P, GROUPS, STAT_WIDTH], F32)
+            with tc.tile_pool(name="work", bufs=2) as work, tc.psum_pool(name="psumT", bufs=2) as psum_t, tc.psum_pool(
+                name="psumB", bufs=4
+            ) as psum_b:
+                planes_of = {}
+                normed_of = {}
+                grouped_of = {}
+                codes_of = {}
 
-                relu_sums = const.tile([P, SUM_CHUNKS, GROUPS], F32)
-                square_sums = const.tile([P, SUM_CHUNKS, GROUPS // SQUARE_SPAN], F32)
-                stats1 = const.tile([P, N_CHUNKS - SUM_CHUNKS, GROUPS, STAT_WIDTH], F32)
-                with tc.tile_pool(name="work", bufs=2) as work, tc.psum_pool(name="psumB", bufs=8) as psum_b:
-                    grouped_of = {}
-                    codes_of = {}
-
-                    def first_norm(g, groups):
-                        cols = slice(g * GROUP, min(g + groups, GROUPS) * GROUP)
+                def turn(g):
+                    pair = [psum_t.tile([P, WORDS, GROUP], BF16, name="planes%d" % u) for u in range(PACK // WORDS)]
+                    for i in range(GROUP_TILES):
                         for t in range(PACK):
-                            nc.vector.tensor_scalar(
-                                out=xT[:, t, cols],
-                                in0=xT[:, t, cols],
-                                scalar1=scale0[:, t : t + 1],
-                                scalar2=shift0[:, t : t + 1],
-                                op0=ALU.mult,
-                                op1=ALU.add,
+                            nc.tensor.transpose(
+                                pair[t // WORDS][:, t % WORDS, i * P : (i + 1) * P],
+                                x_sb[:, g * GROUP_TILES + i, t:K:PACK],
+                                identity_bf[:],
                             )
+                    planes_of[g] = pair
 
-                    def regroup(g):
-                        grouped = work.tile([P, GROUP, PACK], BF16, name="grouped", align_bytes=64)
-                        nc.vector.tensor_copy(
-                            out=grouped[:].rearrange("p (c i) t -> p c t i", i=RUN),
-                            in_=xT[:, :, g * GROUP : (g + 1) * GROUP].rearrange("p t (c i) -> p c t i", i=RUN),
+                def first_norm(g):
+                    normed = work.tile([P, PACK, GROUP], BF16, name="normed")
+                    for t in range(PACK):
+                        nc.vector.tensor_scalar(
+                            out=normed[:, t, :],
+                            in0=planes_of[g][t // WORDS][:, t % WORDS, :],
+                            scalar1=scale0[:, t : t + 1],
+                            scalar2=shift0[:, t : t + 1],
+                            op0=ALU.mult,
+                            op1=ALU.add,
                         )
-                        grouped_of[g] = grouped
+                    normed_of[g] = normed
 
-                    def quantise(g):
-                        codes = work.tile([P, GROUP], U32, name="codes", align_bytes=64)
-                        x_plane = work.tile([P, GROUP], U8, name="x_plane", align_bytes=64)
-                        nc.vector.quantize_mx(
-                            out=codes[:].bitcast(FP8X4),
-                            scales=x_plane[:],
-                            in_=grouped_of[g][:].rearrange("p r t -> p (r t)"),
-                        )
-                        codes_of[g] = (codes, x_plane)
-
-                    def multiply(g):
-                        codes, x_plane = codes_of[g]
-                        for c in range(N_CHUNKS):
-                            n_cols = slice(c * P, (c + 1) * P)
-                            acc = psum_b.tile([P, GROUP], F32, name="acc")
-                            nc.tensor.matmul_mx(
-                                out=acc[:],
-                                lhsT=w_words[:, n_cols].bitcast(FP8X4),
-                                lhsT_scale=w_plane[:, n_cols],
-                                rhs=codes[:].bitcast(FP8X4),
-                                rhs_scale=x_plane[:],
-                                start=True,
-                                stop=True,
-                            )
-                            nc.scalar.activation(
-                                out=h0T[:, c, g * GROUP : (g + 1) * GROUP],
-                                in_=acc[:],
-                                func=ACT.Relu,
-                                bias=vectors[:, 2, c : c + 1],
-                                scale=1.0,
-                                accum_out=relu_sums[:, c, g : g + 1] if c < SUM_CHUNKS else None,
-                            )
-
-                    def hidden_statistics(g):
-                        for c in range(SUM_CHUNKS, N_CHUNKS):
-                            nc.vector.bn_stats(
-                                out=stats1[:, c - SUM_CHUNKS, g, :], in_=h0T[:, c, g * GROUP : (g + 1) * GROUP]
-                            )
-                        if g % SQUARE_SPAN == SQUARE_SPAN - 1:
-                            for c in range(SUM_CHUNKS):
-                                unread = work.tile([P, SQUARE_SPAN * GROUP], BF16, name="unread")
-                                nc.scalar.activation(
-                                    out=unread[:],
-                                    in_=h0T[:, c, (g + 1 - SQUARE_SPAN) * GROUP : (g + 1) * GROUP],
-                                    func=ACT.Square,
-                                    accum_out=square_sums[:, c, g // SQUARE_SPAN : g // SQUARE_SPAN + 1],
-                                )
-
-                    first_norm(0, 1)
-                    for g in range(GROUPS + 2):
-                        if 1 <= g <= GROUPS:
-                            quantise(g - 1)
-                        if g < GROUPS and g % NORM_GROUPS == 1:
-                            first_norm(g, NORM_GROUPS)
-                        if g < GROUPS:
-                            regroup(g)
-                        if 1 <= g <= GROUPS:
-                            multiply(g - 1)
-                        if g >= 2:
-                            hidden_statistics(g - 2)
-
-                    mean_var1 = const.tile([P, N_CHUNKS, 2], F32)
-                    for c in range(SUM_CHUNKS, N_CHUNKS):
-                        nc.vector.bn_aggr(
-                            out=mean_var1[:, c, :], in_=stats1[:, c - SUM_CHUNKS, :, :].rearrange("p a b -> p (a b)")
-                        )
-                    total = const.tile([P, SUM_CHUNKS], F32)
-                    total_sq = const.tile([P, SUM_CHUNKS], F32)
-                    mean_sq = const.tile([P, SUM_CHUNKS], F32)
-                    mean = mean_var1[:, 0:SUM_CHUNKS, 0]
-                    nc.vector.tensor_reduce(out=total[:], in_=relu_sums[:], axis=mybir.AxisListType.X, op=ALU.add)
-                    nc.vector.tensor_scalar(out=mean, in0=total[:], scalar1=1.0 / ROWS, scalar2=None, op0=ALU.mult)
-                    nc.vector.tensor_tensor(out=mean_sq[:], in0=mean, in1=mean, op=ALU.mult)
-                    nc.vector.tensor_reduce(out=total_sq[:], in_=square_sums[:], axis=mybir.AxisListType.X, op=ALU.add)
-                    nc.vector.scalar_tensor_tensor(
-                        out=mean_var1[:, 0:SUM_CHUNKS, 1],
-                        in0=total_sq[:],
-                        scalar=1.0 / ROWS,
-                        in1=mean_sq[:],
-                        op0=ALU.mult,
-                        op1=ALU.subtract,
+                def regroup(g):
+                    grouped = work.tile([P, GROUP, PACK], BF16, name="grouped", align_bytes=64)
+                    nc.vector.tensor_copy(
+                        out=grouped[:].rearrange("p (c i) t -> p c t i", i=RUN),
+                        in_=normed_of[g][:].rearrange("p t (c i) -> p c t i", i=RUN),
                     )
-                    scale1, shift1 = norm_coefficients(nc, const, eps, mean_var1, vectors[:, 3, :], vectors[:, 4, :], "1")
+                    grouped_of[g] = grouped
 
-                with tc.tile_pool(name="stage", bufs=4) as stage, tc.psum_pool(name="psumC", bufs=8) as psum_c:
+                def quantise(g):
+                    codes = work.tile([P, GROUP], U32, name="codes", align_bytes=64)
+                    x_plane = work.tile([P, GROUP], U8, name="x_plane", align_bytes=64)
+                    nc.vector.quantize_mx(
+                        out=codes[:].bitcast(FP8X4),
+                        scales=x_plane[:],
+                        in_=grouped_of[g][:].rearrange("p r t -> p (r t)"),
+                    )
+                    codes_of[g] = (codes, x_plane)
 
-                    def second_norm(first_tile, tiles):
-                        cols = slice(first_tile * P, (first_tile + tiles) * P)
-                        for c in range(N_CHUNKS):
-                            nc.vector.tensor_scalar(
-                                out=h0T[:, c, cols],
-                                in0=h0T[:, c, cols],
-                                scalar1=scale1[:, c : c + 1],
-                                scalar2=shift1[:, c : c + 1],
-                                op0=ALU.mult,
-                                op1=ALU.add,
-                            )
-
-                    firsts = [sum(STORE_TILES[0:s]) for s in range(len(STORE_TILES))]
-                    second_norm(firsts[0], STORE_TILES[0])
-                    for s in range(len(STORE_TILES)):
-                        if s + 1 < len(STORE_TILES):
-                            second_norm(firsts[s + 1], STORE_TILES[s + 1])
-                        result = stage.tile([P, GROUP_TILES, N_OUT], F32, name="result")
-                        for i in range(STORE_TILES[s]):
-                            j = firsts[s] + i
-                            back = psum_c.tile([P, N_OUT], F32, name="back")
-                            for c in range(N_CHUNKS):
-                                nc.tensor.transpose(back[:, c * P : (c + 1) * P], h0T[:, c, j * P : (j + 1) * P], identity[:])
-                            if j % VECTOR_EVERY == VECTOR_EVERY - 1:
-                                nc.vector.tensor_copy(out=result[:, i, :], in_=back[:])
-                            else:
-                                nc.scalar.copy(out=result[:, i, :], in_=back[:])
-                        nc.sync.dma_start(
-                            out=out_rows[:, firsts[s] : firsts[s] + STORE_TILES[s], :], in_=result[:, 0 : STORE_TILES[s], :]
+                def multiply(g):
+                    codes, x_plane = codes_of[g]
+                    for c in range(N_CHUNKS):
+                        n_cols = slice(c * P, (c + 1) * P)
+                        acc = psum_b.tile([P, GROUP], F32, name="acc")
+                        nc.tensor.matmul_mx(
+                            out=acc[:],
+                            lhsT=w_words[:, n_cols].bitcast(FP8X4),
+                            lhsT_scale=w_plane[:, n_cols],
+                            rhs=codes[:].bitcast(FP8X4),
+                            rhs_scale=x_plane[:],
+                            start=True,
+                            stop=True,
                         )
+                        nc.scalar.activation(
+                            out=h0T[:, c, g * GROUP : (g + 1) * GROUP],
+                            in_=acc[:],
+                            func=ACT.Relu,
+                            bias=vectors[:, 2, c : c + 1],
+                            scale=1.0,
+                            accum_out=relu_sums[:, c, g : g + 1] if c != BN_CHUNK else None,
+                        )
+
+                def scalar_squares(c, first, groups):
+                    unread = work.tile([P, 2 * GROUP], BF16, name="unread")
+                    nc.scalar.activation(
+                        out=unread[:, 0 : groups * GROUP],
+                        in_=h0T[:, c, first * GROUP : (first + groups) * GROUP],
+                        func=ACT.Square,
+                        accum_out=square_sums[:, c, first : first + 1],
+                    )
+
+                def hidden_statistics(g):
+                    cols = slice(g * GROUP, (g + 1) * GROUP)
+                    nc.vector.bn_stats(out=stats1[:, g, :], in_=h0T[:, BN_CHUNK, cols])
+                    if g in VECTOR_GROUPS:
+                        unread_v = work.tile([P, GROUP], BF16, name="unread_v")
+                        nc.vector.scalar_tensor_tensor(
+                            out=unread_v[:],
+                            in0=h0T[:, SHARED_CHUNK, cols],
+                            scalar=1.0,
+                            in1=h0T[:, SHARED_CHUNK, cols],
+                            op0=ALU.mult,
+                            op1=ALU.mult,
+                            accum_out=square_sums[:, SHARED_CHUNK, g : g + 1],
+                        )
+                    for first, groups in SPANS:
+                        if first + groups - 1 == g:
+                            for c in range(SHARED_CHUNK):
+                                scalar_squares(c, first, groups)
+                    for first, groups in SHARED_SPANS:
+                        if first + groups - 1 == g:
+                            scalar_squares(SHARED_CHUNK, first, groups)
+
+                turn(0)
+                turn(1)
+                first_norm(0)
+                for g in range(GROUPS + 2):
+                    if 1 <= g <= GROUPS:
+                        quantise(g - 1)
+                    if g < GROUPS:
+                        regroup(g)
+                    if g + 1 < GROUPS:
+                        first_norm(g + 1)
+                    if 1 <= g <= GROUPS:
+                        multiply(g - 1)
+                    if g + 2 < GROUPS:
+                        turn(g + 2)
+                    if g >= 2:
+                        hidden_statistics(g - 2)
+
+                mean_var1 = const.tile([P, N_CHUNKS, 2], F32)
+                total = const.tile([P, SUM_CHUNKS], F32)
+                total_sq = const.tile([P, SUM_CHUNKS], F32)
+                mean_sq = const.tile([P, SUM_CHUNKS], F32)
+                mean = mean_var1[:, 0:SUM_CHUNKS, 0]
+                nc.vector.bn_aggr(out=mean_var1[:, BN_CHUNK, :], in_=stats1[:].rearrange("p a b -> p (a b)"))
+                nc.vector.tensor_reduce(out=total[:], in_=relu_sums[:], axis=mybir.AxisListType.X, op=ALU.add)
+                nc.vector.tensor_scalar(out=mean, in0=total[:], scalar1=1.0 / ROWS, scalar2=None, op0=ALU.mult)
+                nc.vector.tensor_tensor(out=mean_sq[:], in0=mean, in1=mean, op=ALU.mult)
+                nc.vector.tensor_reduce(out=total_sq[:], in_=square_sums[:], axis=mybir.AxisListType.X, op=ALU.add)
+                nc.vector.scalar_tensor_tensor(
+                    out=mean_var1[:, 0:SUM_CHUNKS, 1],
+                    in0=total_sq[:],
+                    scalar=1.0 / ROWS,
+                    in1=mean_sq[:],
+                    op0=ALU.mult,
+                    op1=ALU.subtract,
+                )
+                scale1, shift1 = norm_coefficients(nc, const, eps, mean_var1, vectors[:, 3, :], vectors[:, 4, :], "1")
+
+            with tc.tile_pool(name="stage", bufs=4) as stage, tc.psum_pool(name="psumC", bufs=8) as psum_c:
+
+                def second_norm(first_tile, tiles):
+                    cols = slice(first_tile * P, (first_tile + tiles) * P)
+                    for c in range(N_CHUNKS):
+                        nc.vector.tensor_scalar(
+                            out=h0T[:, c, cols],
+                            in0=h0T[:, c, cols],
+                            scalar1=scale1[:, c : c + 1],
+                            scalar2=shift1[:, c : c + 1],
+                            op0=ALU.mult,
+                            op1=ALU.add,
+                        )
+
+                firsts = [sum(STORE_TILES[0:s]) for s in range(len(STORE_TILES))]
+                second_norm(firsts[0], STORE_TILES[0])
+                for s in range(len(STORE_TILES)):
+                    if s + 1 < len(STORE_TILES):
+                        second_norm(firsts[s + 1], STORE_TILES[s + 1])
+                    result = stage.tile([P, GROUP_TILES, N_OUT], F32, name="result")
+                    for i in range(STORE_TILES[s]):
+                        j = firsts[s] + i
+                        back = psum_c.tile([P, N_OUT], F32, name="back")
+                        for c in range(N_CHUNKS):
+                            nc.tensor.transpose(back[:, c * P : (c + 1) * P], h0T[:, c, j * P : (j + 1) * P], identity[:])
+                        if j % VECTOR_EVERY == VECTOR_EVERY - 1:
+                            nc.vector.tensor_copy(out=result[:, i, :], in_=back[:])
+                        else:
+                            nc.scalar.copy(out=result[:, i, :], in_=back[:])
+                    nc.sync.dma_start(
+                        out=out_rows[:, firsts[s] : firsts[s] + STORE_TILES[s], :], in_=result[:, 0 : STORE_TILES[s], :]
+                    )

@@ -121,7 +121,8 @@ def tile_settransform_pa_kernel(tc, set_feats, g0, b0, W0_words, W0_scales, c0, 
                         words = x_sb[:, j, :].bitcast(F32)
                         nc.tensor.transpose(bank_v[:, i * P : (i + 1) * P], words[:, 0 : K // HALVES : WORDS], identity[:])
                         nc.tensor.transpose(bank_a[:, i * P : (i + 1) * P], words[:, 1 : K // HALVES : WORDS], identity[:])
-                        for e in range(HALVES):
+                    for e in range(HALVES):
+                        for j in range(s * STAT_TILES, (s + 1) * STAT_TILES):
                             nc.tensor.matmul(
                                 out=sums[e][:, 0:1],
                                 lhsT=x_sb[:, j, HALVES * SCALAR_WORD + e : K : PACK],

@@ -37,11 +37,11 @@ GROUPS = ROWS // GROUP
 RUN = 4
 
 BN_CHUNK = 3
+CHUNK_ORDER = (3, 2, 0, 1)
 SHARED_CHUNK = 2
 SUM_CHUNKS = 3
 VECTOR_GROUPS = (2, 5, 8, 11, 14, 15)
-SPANS = tuple((g, 2) for g in range(0, 14, 2)) + ((14, 1), (15, 1))
-SHARED_SPANS = tuple((g, 2) for g in range(0, 14, 3))
+WARM_UP = 6
 
 VECTOR_EVERY = 4
 STORE_TILES = (1, 1, 2) + (4,) * 15
@@ -172,29 +172,37 @@ def tile_settransform_pa_kernel(tc, set_feats, g0, b0, W0_words, W0_scales, c0, 
                 grouped_of = {}
                 codes_of = {}
 
-                def turn(g):
-                    pair = [psum_t.tile([P, WORDS, GROUP], BF16, name="planes%d" % u) for u in range(PACK // WORDS)]
-                    for i in range(GROUP_TILES):
+                def open_planes(g):
+                    planes_of[g] = [psum_t.tile([P, WORDS, GROUP], BF16, name="planes%d" % u) for u in range(PACK // WORDS)]
+
+                def hold_clock(g):
+                    unread_bank = planes_of[g][1][:].rearrange("p u r -> p (u r)").bitcast(F32)
+                    nc.tensor.matmul(
+                        out=unread_bank[:, GROUP - P : GROUP], lhsT=identity[:], rhs=identity[:], start=True, stop=True
+                    )
+
+                def turn(g, tiles):
+                    for i in tiles:
                         for t in range(PACK):
                             nc.tensor.transpose(
-                                pair[t // WORDS][:, t % WORDS, i * P : (i + 1) * P],
+                                planes_of[g][t // WORDS][:, t % WORDS, i * P : (i + 1) * P],
                                 x_sb[:, g * GROUP_TILES + i, t:K:PACK],
                                 identity_bf[:],
                             )
-                    planes_of[g] = pair
 
-                def first_norm(g):
-                    normed = work.tile([P, PACK, GROUP], BF16, name="normed")
-                    for t in range(PACK):
+                def first_norm(g, planes=range(PACK)):
+                    for t in planes:
                         nc.vector.tensor_scalar(
-                            out=normed[:, t, :],
+                            out=normed_of[g][:, t, :],
                             in0=planes_of[g][t // WORDS][:, t % WORDS, :],
                             scalar1=scale0[:, t : t + 1],
                             scalar2=shift0[:, t : t + 1],
                             op0=ALU.mult,
                             op1=ALU.add,
                         )
-                    normed_of[g] = normed
+
+                def normed_tile(g):
+                    normed_of[g] = work.tile([P, PACK, GROUP], BF16, name="normed")
 
                 def regroup(g):
                     grouped = work.tile([P, GROUP, PACK], BF16, name="grouped", align_bytes=64)
@@ -214,9 +222,9 @@ def tile_settransform_pa_kernel(tc, set_feats, g0, b0, W0_words, W0_scales, c0, 
                     )
                     codes_of[g] = (codes, x_plane)
 
-                def multiply(g):
+                def multiply(g, chunks):
                     codes, x_plane = codes_of[g]
-                    for c in range(N_CHUNKS):
+                    for c in chunks:
                         n_cols = slice(c * P, (c + 1) * P)
                         acc = psum_b.tile([P, GROUP], F32, name="acc")
                         nc.tensor.matmul_mx(
@@ -246,42 +254,74 @@ def tile_settransform_pa_kernel(tc, set_feats, g0, b0, W0_words, W0_scales, c0, 
                         accum_out=square_sums[:, c, first : first + 1],
                     )
 
-                def hidden_statistics(g):
-                    cols = slice(g * GROUP, (g + 1) * GROUP)
-                    nc.vector.bn_stats(out=stats1[:, g, :], in_=h0T[:, BN_CHUNK, cols])
-                    if g in VECTOR_GROUPS:
-                        unread_v = work.tile([P, GROUP], BF16, name="unread_v")
-                        nc.vector.scalar_tensor_tensor(
-                            out=unread_v[:],
-                            in0=h0T[:, SHARED_CHUNK, cols],
-                            scalar=1.0,
-                            in1=h0T[:, SHARED_CHUNK, cols],
-                            op0=ALU.mult,
-                            op1=ALU.mult,
-                            accum_out=square_sums[:, SHARED_CHUNK, g : g + 1],
-                        )
-                    for first, groups in SPANS:
-                        if first + groups - 1 == g:
-                            for c in range(SHARED_CHUNK):
-                                scalar_squares(c, first, groups)
-                    for first, groups in SHARED_SPANS:
-                        if first + groups - 1 == g:
-                            scalar_squares(SHARED_CHUNK, first, groups)
+                def vector_squares(c, g):
+                    h = h0T[:, c, g * GROUP : (g + 1) * GROUP]
+                    unread_v = work.tile([P, GROUP], BF16, name="unread_v")
+                    nc.vector.scalar_tensor_tensor(
+                        out=unread_v[:],
+                        in0=h,
+                        scalar=1.0,
+                        in1=h,
+                        op0=ALU.mult,
+                        op1=ALU.mult,
+                        accum_out=square_sums[:, c, g : g + 1],
+                    )
 
-                turn(0)
-                turn(1)
-                first_norm(0)
-                for g in range(GROUPS + 2):
-                    if 1 <= g <= GROUPS:
+                def hidden_statistics(g):
+                    nc.vector.bn_stats(out=stats1[:, g, :], in_=h0T[:, BN_CHUNK, g * GROUP : (g + 1) * GROUP])
+                    if g in VECTOR_GROUPS:
+                        vector_squares(SHARED_CHUNK, g)
+                    else:
+                        scalar_squares(SHARED_CHUNK, g, 1)
+                    if g == GROUPS - 1:
+                        vector_squares(0, g)
+                    elif g == GROUPS - 2:
+                        scalar_squares(0, g, 1)
+                    elif g % 2 == 1:
+                        scalar_squares(0, g - 1, 2)
+                    if g == 0 or g == GROUPS - 1:
+                        scalar_squares(1, g, 1)
+                    elif g % 2 == 0:
+                        scalar_squares(1, g - 1, 2)
+
+                for g in range(2):
+                    open_planes(g)
+                    for i in range(WARM_UP // 2):
+                        hold_clock(g)
+                    turn(g, range(GROUP_TILES))
+                normed_tile(0)
+                first_norm(0, range(WORDS))
+                for t in range(WORDS, PACK):
+                    nc.scalar.activation(
+                        out=normed_of[0][:, t, :],
+                        in_=planes_of[0][t // WORDS][:, t % WORDS, :],
+                        func=ACT.Identity,
+                        scale=scale0[:, t : t + 1],
+                        bias=shift0[:, t : t + 1],
+                    )
+                open_planes(2)
+                hold_clock(2)
+                turn(2, range(GROUP_TILES))
+                regroup(0)
+                quantise(0)
+                normed_tile(1)
+                first_norm(1)
+                for g in range(1, GROUPS + 2):
+                    if 2 <= g <= GROUPS:
                         quantise(g - 1)
                     if g < GROUPS:
                         regroup(g)
                     if g + 1 < GROUPS:
+                        normed_tile(g + 1)
                         first_norm(g + 1)
-                    if 1 <= g <= GROUPS:
-                        multiply(g - 1)
                     if g + 2 < GROUPS:
-                        turn(g + 2)
+                        open_planes(g + 2)
+                    for half in range(2):
+                        if g <= GROUPS:
+                            multiply(g - 1, CHUNK_ORDER[2 * half : 2 * half + 2])
+                        if g + 2 < GROUPS:
+                            hold_clock(g + 2)
+                            turn(g + 2, range(2 * half, 2 * half + 2))
                     if g >= 2:
                         hidden_statistics(g - 2)
 

@@ -29,6 +29,7 @@ STAT_ROWS = 512
 STAT_TILES = STAT_ROWS // P
 STAT_GROUPS = ROWS // STAT_ROWS
 STAT_WIDTH = 6
+SUMS_AFTER = (3, 7, 11, 14, 15)
 SCALAR_WORD = 1
 
 GROUP = 512
@@ -40,9 +41,7 @@ BN_CHUNK = 3
 CHUNK_ORDER = (3, 2, 0, 1)
 SHARED_CHUNK = 2
 SUM_CHUNKS = 3
-VECTOR_GROUPS = (2, 5, 8, 11, 14, 15)
-WARM_UP = 6
-
+VECTOR_GROUPS = (2, 4, 6, 8, 10, 12, 14, 15)
 VECTOR_EVERY = 4
 STORE_TILES = (1, 1, 2) + (4,) * 15
 
@@ -113,6 +112,7 @@ def tile_settransform_pa_kernel(tc, set_feats, g0, b0, W0_words, W0_scales, c0, 
                     nc.sync.dma_start(out=vectors_bf[:, 3, 0:N_CHUNKS], in_=g1.rearrange("(c p) -> p c", p=P))
                     nc.sync.dma_start(out=vectors_bf[:, 4, 0:N_CHUNKS], in_=b1.rearrange("(c p) -> p c", p=P))
 
+                summed = 0
                 for s in range(STAT_GROUPS):
                     bank_v = psum_v.tile([P, STAT_ROWS], F32, name="bank_v")
                     bank_a = psum_a.tile([P, STAT_ROWS], F32, name="bank_a")
@@ -121,8 +121,8 @@ def tile_settransform_pa_kernel(tc, set_feats, g0, b0, W0_words, W0_scales, c0, 
                         words = x_sb[:, j, :].bitcast(F32)
                         nc.tensor.transpose(bank_v[:, i * P : (i + 1) * P], words[:, 0 : K // HALVES : WORDS], identity[:])
                         nc.tensor.transpose(bank_a[:, i * P : (i + 1) * P], words[:, 1 : K // HALVES : WORDS], identity[:])
-                    for e in range(HALVES):
-                        for j in range(s * STAT_TILES, (s + 1) * STAT_TILES):
+                    for e in range(HALVES if s in SUMS_AFTER else 0):
+                        for j in range(summed, (s + 1) * STAT_TILES):
                             nc.tensor.matmul(
                                 out=sums[e][:, 0:1],
                                 lhsT=x_sb[:, j, HALVES * SCALAR_WORD + e : K : PACK],
@@ -130,6 +130,8 @@ def tile_settransform_pa_kernel(tc, set_feats, g0, b0, W0_words, W0_scales, c0, 
                                 start=(j == 0),
                                 stop=(j == ROW_TILES - 1),
                             )
+                    if s in SUMS_AFTER:
+                        summed = (s + 1) * STAT_TILES
                     halves_v = bank_v[:].bitcast(BF16).rearrange("p (r e) -> p e r", e=HALVES)
                     halves_a = bank_a[:].bitcast(BF16).rearrange("p (r e) -> p e r", e=HALVES)
                     for e in range(HALVES):
@@ -175,14 +177,8 @@ def tile_settransform_pa_kernel(tc, set_feats, g0, b0, W0_words, W0_scales, c0, 
                 def open_planes(g):
                     planes_of[g] = [psum_t.tile([P, WORDS, GROUP], BF16, name="planes%d" % u) for u in range(PACK // WORDS)]
 
-                def hold_clock(g):
-                    unread_bank = planes_of[g][1][:].rearrange("p u r -> p (u r)").bitcast(F32)
-                    nc.tensor.matmul(
-                        out=unread_bank[:, GROUP - P : GROUP], lhsT=identity[:], rhs=identity[:], start=True, stop=True
-                    )
-
-                def turn(g, tiles):
-                    for i in tiles:
+                def turn(g):
+                    for i in range(GROUP_TILES):
                         for t in range(PACK):
                             nc.tensor.transpose(
                                 planes_of[g][t // WORDS][:, t % WORDS, i * P : (i + 1) * P],
@@ -222,9 +218,9 @@ def tile_settransform_pa_kernel(tc, set_feats, g0, b0, W0_words, W0_scales, c0, 
                     )
                     codes_of[g] = (codes, x_plane)
 
-                def multiply(g, chunks):
+                def multiply(g):
                     codes, x_plane = codes_of[g]
-                    for c in chunks:
+                    for c in CHUNK_ORDER:
                         n_cols = slice(c * P, (c + 1) * P)
                         acc = psum_b.tile([P, GROUP], F32, name="acc")
                         nc.tensor.matmul_mx(
@@ -275,20 +271,21 @@ def tile_settransform_pa_kernel(tc, set_feats, g0, b0, W0_words, W0_scales, c0, 
                         scalar_squares(SHARED_CHUNK, g, 1)
                     if g == GROUPS - 1:
                         vector_squares(0, g)
-                    elif g == GROUPS - 2:
-                        scalar_squares(0, g, 1)
-                    elif g % 2 == 1:
-                        scalar_squares(0, g - 1, 2)
-                    if g == 0 or g == GROUPS - 1:
                         scalar_squares(1, g, 1)
-                    elif g % 2 == 0:
-                        scalar_squares(1, g - 1, 2)
+                    elif g == GROUPS - 2:
+                        vector_squares(0, g)
+                        vector_squares(1, g)
+                    else:
+                        if g % 2 == 1:
+                            scalar_squares(0, g - 1, 2)
+                        if g == 0 or g == GROUPS - 3:
+                            scalar_squares(1, g, 1)
+                        elif g % 2 == 0:
+                            scalar_squares(1, g - 1, 2)
 
                 for g in range(2):
                     open_planes(g)
-                    for i in range(WARM_UP // 2):
-                        hold_clock(g)
-                    turn(g, range(GROUP_TILES))
+                    turn(g)
                 normed_tile(0)
                 first_norm(0, range(WORDS))
                 for t in range(WORDS, PACK):
@@ -300,8 +297,7 @@ def tile_settransform_pa_kernel(tc, set_feats, g0, b0, W0_words, W0_scales, c0, 
                         bias=shift0[:, t : t + 1],
                     )
                 open_planes(2)
-                hold_clock(2)
-                turn(2, range(GROUP_TILES))
+                turn(2)
                 regroup(0)
                 quantise(0)
                 normed_tile(1)
@@ -316,12 +312,10 @@ def tile_settransform_pa_kernel(tc, set_feats, g0, b0, W0_words, W0_scales, c0, 
                         first_norm(g + 1)
                     if g + 2 < GROUPS:
                         open_planes(g + 2)
-                    for half in range(2):
-                        if g <= GROUPS:
-                            multiply(g - 1, CHUNK_ORDER[2 * half : 2 * half + 2])
-                        if g + 2 < GROUPS:
-                            hold_clock(g + 2)
-                            turn(g + 2, range(2 * half, 2 * half + 2))
+                    if g <= GROUPS:
+                        multiply(g - 1)
+                    if g + 2 < GROUPS:
+                        turn(g + 2)
                     if g >= 2:
                         hidden_statistics(g - 2)
 

import concourse.mybir as mybir
from concourse.masks import make_identity

FLOPS = 2 * 8192 * 512 * 512

F32 = mybir.dt.float32
BF16 = mybir.dt.bfloat16
I32 = mybir.dt.int32
U32 = mybir.dt.uint32
U8 = mybir.dt.uint8
FP8X4 = mybir.dt.float8_e4m3fn_x4
ALU = mybir.AluOpType
ACT = mybir.ActivationFunctionType

P = 128
PACK = 4
HALVES = 2
WORDS = PACK // HALVES
ROWS = 8192
K = 512
N_OUT = 512
N_CHUNKS = N_OUT // P
ROW_TILES = ROWS // P
EPS = 1e-5

LOAD_TILES = 4
FIRST_LOADS = (1, 1, 2)
STAT_ROWS = 512
STAT_TILES = STAT_ROWS // P
STAT_GROUPS = ROWS // STAT_ROWS
STAT_WIDTH = 6
SUMS_AFTER = (3, 7, 11, 14, 15)
SCALAR_WORD = 1

GROUP = 512
GROUP_TILES = GROUP // P
GROUPS = ROWS // GROUP
RUN = 4

BN_CHUNK = 3
CHUNK_ORDER = (3, 2, 0, 1)
SHARED_CHUNK = 2
SUM_CHUNKS = 3
VECTOR_GROUPS = (2, 4, 6, 8, 10, 12, 14, 15)
VECTOR_EVERY = 4
STORE_TILES = (1, 1, 2) + (4,) * 15

def norm_coefficients(nc, pool, eps, mean_var, gain, shift_in, label):
    width = gain.shape[1]
    rstd = pool.tile([P, width], F32, name="rstd" + label)
    scale = pool.tile([P, width], F32, name="scale" + label)
    shift = pool.tile([P, width], F32, name="shift" + label)
    nc.scalar.activation(out=rstd[:], in_=mean_var[:, :, 1], func=ACT.Abs_reciprocal_sqrt, bias=eps[:], scale=1.0)
    nc.vector.tensor_tensor(out=scale[:], in0=rstd[:], in1=gain, op=ALU.mult)
    nc.vector.tensor_tensor(out=shift[:], in0=mean_var[:, :, 0], in1=scale[:], op=ALU.mult)
    nc.vector.tensor_tensor(out=shift[:], in0=shift_in, in1=shift[:], op=ALU.subtract)
    return scale, shift


def tile_settransform_pa_kernel(tc, set_feats, g0, b0, W0_words, W0_scales, c0, g1, b1, out):
    nc = tc.nc
    x_rows = set_feats.rearrange("b s k -> (b s) k").rearrange("(p j) k -> p j k", j=ROW_TILES)
    out_rows = out.rearrange("b s n -> (b s) n").rearrange("(p j) n -> p j n", j=ROW_TILES)

    with tc.manual_schedule(), tc.tile_pool(name="const", bufs=1) as const:
        identity = const.tile([P, P], F32)
        make_identity(nc, identity[:])
        identity_bf = const.tile([P, P], BF16)
        make_identity(nc, identity_bf[:])
        ones = const.tile([P, 1], BF16)
        nc.vector.memset(ones[:], 1.0)
        warm = const.tile([P, 1], F32)
        nc.vector.memset(warm[:], 1.0)
        nc.scalar.activation(out=warm[:], in_=warm[:], func=ACT.Abs_reciprocal_sqrt)
        eps = const.tile([P, 1], F32)
        nc.vector.memset(eps[:], EPS)

        w_words = const.tile([P, N_OUT], U32, align_bytes=64)
        w_plane = const.tile([P, N_OUT], U8, align_bytes=64)
        nc.vector.memset(w_plane[:].bitcast(I32), 0)

        with tc.tile_pool(name="x", bufs=1) as x_pool, tc.tile_pool(name="hidden", bufs=1) as hidden:
            x_sb = x_pool.tile([P, ROW_TILES, K], BF16)
            h0T = hidden.tile([P, N_CHUNKS, ROWS], F32)

            stats0 = const.tile([P, HALVES, STAT_GROUPS, STAT_WIDTH], F32)
            squares0 = const.tile([P, HALVES, STAT_GROUPS], F32)
            mean_var0 = const.tile([P, PACK, 2], F32)
            with tc.psum_pool(name="psumV", bufs=3) as psum_v, tc.psum_pool(name="psumA", bufs=3) as psum_a, tc.psum_pool(
                name="psumS", bufs=1
            ) as psum_s, tc.tile_pool(name="junk", bufs=2) as junk:
                sums = [psum_s.tile([P, 512], F32, name="sum%d" % e) for e in range(HALVES)]
                sizes = list(FIRST_LOADS) + [LOAD_TILES] * ((ROW_TILES - sum(FIRST_LOADS)) // LOAD_TILES)
                j = 0
                for size in sizes:
                    nc.sync.dma_start(out=x_sb[:, j : j + size, :], in_=x_rows[:, j : j + size, :])
                    j += size
                nc.sync.dma_start(
                    out=w_words[:].bitcast(I32), in_=W0_words[0].rearrange("p n t -> p (n t)").bitcast(I32)
                )
                for quadrant in range(4):
                    nc.sync.dma_start(
                        out=w_plane[32 * quadrant : 32 * quadrant + 4, :].bitcast(I32),
                        in_=W0_scales[0, 4 * quadrant : 4 * quadrant + 4, :].bitcast(I32),
                    )
                vectors_bf = const.tile([P, 5, 16], BF16)
                vectors = const.tile([P, 5, PACK], F32)
                with nc.allow_non_contiguous_dma(reason="five vectors of 512 values, four to a partition"):
                    nc.sync.dma_start(out=vectors_bf[:, 0, 0:PACK], in_=g0.rearrange("(p t) -> p t", t=PACK))
                    nc.sync.dma_start(out=vectors_bf[:, 1, 0:PACK], in_=b0.rearrange("(p t) -> p t", t=PACK))
                    nc.sync.dma_start(out=vectors_bf[:, 2, 0:N_CHUNKS], in_=c0.rearrange("(c p) -> p c", p=P))
                    nc.sync.dma_start(out=vectors_bf[:, 3, 0:N_CHUNKS], in_=g1.rearrange("(c p) -> p c", p=P))
                    nc.sync.dma_start(out=vectors_bf[:, 4, 0:N_CHUNKS], in_=b1.rearrange("(c p) -> p c", p=P))

                summed = 0
                for s in range(STAT_GROUPS):
                    bank_v = psum_v.tile([P, STAT_ROWS], F32, name="bank_v")
                    bank_a = psum_a.tile([P, STAT_ROWS], F32, name="bank_a")
                    for i in range(STAT_TILES):
                        j = s * STAT_TILES + i
                        words = x_sb[:, j, :].bitcast(F32)
                        nc.tensor.transpose(bank_v[:, i * P : (i + 1) * P], words[:, 0 : K // HALVES : WORDS], identity[:])
                        nc.tensor.transpose(bank_a[:, i * P : (i + 1) * P], words[:, 1 : K // HALVES : WORDS], identity[:])
                    for e in range(HALVES if s in SUMS_AFTER else 0):
                        for j in range(summed, (s + 1) * STAT_TILES):
                            nc.tensor.matmul(
                                out=sums[e][:, 0:1],
                                lhsT=x_sb[:, j, HALVES * SCALAR_WORD + e : K : PACK],
                                rhs=ones[:],
                                start=(j == 0),
                                stop=(j == ROW_TILES - 1),
                            )
                    if s in SUMS_AFTER:
                        summed = (s + 1) * STAT_TILES
                    halves_v = bank_v[:].bitcast(BF16).rearrange("p (r e) -> p e r", e=HALVES)
                    halves_a = bank_a[:].bitcast(BF16).rearrange("p (r e) -> p e r", e=HALVES)
                    for e in range(HALVES):
                        nc.vector.bn_stats(out=stats0[:, e, s, :], in_=halves_v[:, e, :])
                        unread0 = junk.tile([P, STAT_ROWS], BF16, name="unread0")
                        nc.scalar.activation(
                            out=unread0[:], in_=halves_a[:, e, :], func=ACT.Square, accum_out=squares0[:, e, s : s + 1]
                        )
                nc.vector.tensor_copy(out=vectors[:], in_=vectors_bf[:, :, 0:PACK])
                for e in range(HALVES):
                    nc.vector.bn_aggr(out=mean_var0[:, e, :], in_=stats0[:, e, :, :].rearrange("p a b -> p (a b)"))
                total_sq0 = const.tile([P, HALVES], F32)
                mean_sq0 = const.tile([P, HALVES], F32)
                mean0 = mean_var0[:, HALVES:PACK, 0]
                for e in range(HALVES):
                    nc.vector.tensor_scalar(
                        out=mean_var0[:, HALVES + e, 0:1], in0=sums[e][:, 0:1], scalar1=1.0 / ROWS, scalar2=None, op0=ALU.mult
                    )
                nc.vector.tensor_reduce(out=total_sq0[:], in_=squares0[:], axis=mybir.AxisListType.X, op=ALU.add)
                nc.vector.tensor_tensor(out=mean_sq0[:], in0=mean0, in1=mean0, op=ALU.mult)
                nc.vector.scalar_tensor_tensor(
                    out=mean_var0[:, HALVES:PACK, 1],
                    in0=total_sq0[:],
                    scalar=1.0 / ROWS,
                    in1=mean_sq0[:],
                    op0=ALU.mult,
                    op1=ALU.subtract,
                )
                scale0, shift0 = norm_coefficients(nc, const, eps, mean_var0, vectors[:, 0, :], vectors[:, 1, :], "0")

            relu_sums = const.tile([P, SUM_CHUNKS, GROUPS], F32)
            square_sums = const.tile([P, SUM_CHUNKS, GROUPS], F32)
            nc.vector.memset(square_sums[:], 0.0)
            stats1 = const.tile([P, GROUPS, STAT_WIDTH], F32)
            with tc.tile_pool(name="work", bufs=2) as work, tc.psum_pool(name="psumT", bufs=2) as psum_t, tc.psum_pool(
                name="psumB", bufs=4
            ) as psum_b:
                planes_of = {}
                normed_of = {}
                grouped_of = {}
                codes_of = {}

                def open_planes(g):
                    planes_of[g] = [psum_t.tile([P, WORDS, GROUP], BF16, name="planes%d" % u) for u in range(PACK // WORDS)]

                def turn(g):
                    for i in range(GROUP_TILES):
                        for t in range(PACK):
                            nc.tensor.transpose(
                                planes_of[g][t // WORDS][:, t % WORDS, i * P : (i + 1) * P],
                                x_sb[:, g * GROUP_TILES + i, t:K:PACK],
                                identity_bf[:],
                            )

                def first_norm(g, planes=range(PACK)):
                    for t in planes:
                        nc.vector.tensor_scalar(
                            out=normed_of[g][:, t, :],
                            in0=planes_of[g][t // WORDS][:, t % WORDS, :],
                            scalar1=scale0[:, t : t + 1],
                            scalar2=shift0[:, t : t + 1],
                            op0=ALU.mult,
                            op1=ALU.add,
                        )

                def normed_tile(g):
                    normed_of[g] = work.tile([P, PACK, GROUP], BF16, name="normed")

                def regroup(g):
                    grouped = work.tile([P, GROUP, PACK], BF16, name="grouped", align_bytes=64)
                    nc.vector.tensor_copy(
                        out=grouped[:].rearrange("p (c i) t -> p c t i", i=RUN),
                        in_=normed_of[g][:].rearrange("p t (c i) -> p c t i", i=RUN),
                    )
                    grouped_of[g] = grouped

                def quantise(g):
                    codes = work.tile([P, GROUP], U32, name="codes", align_bytes=64)
                    x_plane = work.tile([P, GROUP], U8, name="x_plane", align_bytes=64)
                    nc.vector.quantize_mx(
                        out=codes[:].bitcast(FP8X4),
                        scales=x_plane[:],
                        in_=grouped_of[g][:].rearrange("p r t -> p (r t)"),
                    )
                    codes_of[g] = (codes, x_plane)

                def multiply(g):
                    codes, x_plane = codes_of[g]
                    for c in CHUNK_ORDER:
                        n_cols = slice(c * P, (c + 1) * P)
                        acc = psum_b.tile([P, GROUP], F32, name="acc")
                        nc.tensor.matmul_mx(
                            out=acc[:],
                            lhsT=w_words[:, n_cols].bitcast(FP8X4),
                            lhsT_scale=w_plane[:, n_cols],
                            rhs=codes[:].bitcast(FP8X4),
                            rhs_scale=x_plane[:],
                            start=True,
                            stop=True,
                        )
                        nc.scalar.activation(
                            out=h0T[:, c, g * GROUP : (g + 1) * GROUP],
                            in_=acc[:],
                            func=ACT.Relu,
                            bias=vectors[:, 2, c : c + 1],
                            scale=1.0,
                            accum_out=relu_sums[:, c, g : g + 1] if c != BN_CHUNK else None,
                        )

                def scalar_squares(c, first, groups):
                    unread = work.tile([P, 2 * GROUP], BF16, name="unread")
                    nc.scalar.activation(
                        out=unread[:, 0 : groups * GROUP],
                        in_=h0T[:, c, first * GROUP : (first + groups) * GROUP],
                        func=ACT.Square,
                        accum_out=square_sums[:, c, first : first + 1],
                    )

                def vector_squares(c, g):
                    h = h0T[:, c, g * GROUP : (g + 1) * GROUP]
                    unread_v = work.tile([P, GROUP], BF16, name="unread_v")
                    nc.vector.scalar_tensor_tensor(
                        out=unread_v[:],
                        in0=h,
                        scalar=1.0,
                        in1=h,
                        op0=ALU.mult,
                        op1=ALU.mult,
                        accum_out=square_sums[:, c, g : g + 1],
                    )

                def hidden_statistics(g):
                    nc.vector.bn_stats(out=stats1[:, g, :], in_=h0T[:, BN_CHUNK, g * GROUP : (g + 1) * GROUP])
                    if g in VECTOR_GROUPS:
                        vector_squares(SHARED_CHUNK, g)
                    else:
                        scalar_squares(SHARED_CHUNK, g, 1)
                    if g == GROUPS - 1:
                        vector_squares(0, g)
                        scalar_squares(1, g, 1)
                    elif g == GROUPS - 2:
                        vector_squares(0, g)
                        vector_squares(1, g)
                    else:
                        if g % 2 == 1:
                            scalar_squares(0, g - 1, 2)
                        if g == 0 or g == GROUPS - 3:
                            scalar_squares(1, g, 1)
                        elif g % 2 == 0:
                            scalar_squares(1, g - 1, 2)

                for g in range(2):
                    open_planes(g)
                    turn(g)
                normed_tile(0)
                first_norm(0, range(WORDS))
                for t in range(WORDS, PACK):
                    nc.scalar.activation(
                        out=normed_of[0][:, t, :],
                        in_=planes_of[0][t // WORDS][:, t % WORDS, :],
                        func=ACT.Identity,
                        scale=scale0[:, t : t + 1],
                        bias=shift0[:, t : t + 1],
                    )
                open_planes(2)
                turn(2)
                regroup(0)
                quantise(0)
                normed_tile(1)
                first_norm(1)
                for g in range(1, GROUPS + 2):
                    if 2 <= g <= GROUPS:
                        quantise(g - 1)
                    if g < GROUPS:
                        regroup(g)
                    if g + 1 < GROUPS:
                        normed_tile(g + 1)
                        first_norm(g + 1)
                    if g + 2 < GROUPS:
                        open_planes(g + 2)
                    if g <= GROUPS:
                        multiply(g - 1)
                    if g + 2 < GROUPS:
                        turn(g + 2)
                    if g >= 2:
                        hidden_statistics(g - 2)

                mean_var1 = const.tile([P, N_CHUNKS, 2], F32)
                total = const.tile([P, SUM_CHUNKS], F32)
                total_sq = const.tile([P, SUM_CHUNKS], F32)
                mean_sq = const.tile([P, SUM_CHUNKS], F32)
                mean = mean_var1[:, 0:SUM_CHUNKS, 0]
                nc.vector.bn_aggr(out=mean_var1[:, BN_CHUNK, :], in_=stats1[:].rearrange("p a b -> p (a b)"))
                nc.vector.tensor_reduce(out=total[:], in_=relu_sums[:], axis=mybir.AxisListType.X, op=ALU.add)
                nc.vector.tensor_scalar(out=mean, in0=total[:], scalar1=1.0 / ROWS, scalar2=None, op0=ALU.mult)
                nc.vector.tensor_tensor(out=mean_sq[:], in0=mean, in1=mean, op=ALU.mult)
                nc.vector.tensor_reduce(out=total_sq[:], in_=square_sums[:], axis=mybir.AxisListType.X, op=ALU.add)
                nc.vector.scalar_tensor_tensor(
                    out=mean_var1[:, 0:SUM_CHUNKS, 1],
                    in0=total_sq[:],
                    scalar=1.0 / ROWS,
                    in1=mean_sq[:],
                    op0=ALU.mult,
                    op1=ALU.subtract,
                )
                scale1, shift1 = norm_coefficients(nc, const, eps, mean_var1, vectors[:, 3, :], vectors[:, 4, :], "1")

            with tc.tile_pool(name="stage", bufs=4) as stage, tc.psum_pool(name="psumC", bufs=8) as psum_c:

                def second_norm(first_tile, tiles):
                    cols = slice(first_tile * P, (first_tile + tiles) * P)
                    for c in range(N_CHUNKS):
                        nc.vector.tensor_scalar(
                            out=h0T[:, c, cols],
                            in0=h0T[:, c, cols],
                            scalar1=scale1[:, c : c + 1],
                            scalar2=shift1[:, c : c + 1],
                            op0=ALU.mult,
                            op1=ALU.add,
                        )

                firsts = [sum(STORE_TILES[0:s]) for s in range(len(STORE_TILES))]
                second_norm(firsts[0], STORE_TILES[0])
                for s in range(len(STORE_TILES)):
                    if s + 1 < len(STORE_TILES):
                        second_norm(firsts[s + 1], STORE_TILES[s + 1])
                    result = stage.tile([P, GROUP_TILES, N_OUT], F32, name="result")
                    for i in range(STORE_TILES[s]):
                        j = firsts[s] + i
                        back = psum_c.tile([P, N_OUT], F32, name="back")
                        for c in range(N_CHUNKS):
                            nc.tensor.transpose(back[:, c * P : (c + 1) * P], h0T[:, c, j * P : (j + 1) * P], identity[:])
                        if j % VECTOR_EVERY == VECTOR_EVERY - 1:
                            nc.vector.tensor_copy(out=result[:, i, :], in_=back[:])
                        else:
                            nc.scalar.copy(out=result[:, i, :], in_=back[:])
                    nc.sync.dma_start(
                        out=out_rows[:, firsts[s] : firsts[s] + STORE_TILES[s], :], in_=result[:, 0 : STORE_TILES[s], :]
                    )
